import numpy as np
import ml_dtypes


def mxq(x, axis, fmt="e4m3"):
    dtype, down = {"e4m3": (ml_dtypes.float8_e4m3fn, 7), "e5m2": (ml_dtypes.float8_e5m2, 14)}[fmt]
    v = np.moveaxis(np.asarray(x, np.float32).astype(ml_dtypes.bfloat16).astype(np.float64), axis, -1)
    blocks = v.reshape(v.shape[:-1] + (-1, 32))
    amax = np.abs(blocks).max(-1, keepdims=True)
    byte = np.maximum(np.where(amax > 0, np.frexp(amax)[1] - 1 + 127, 0) - down, 1)
    scale = np.exp2(byte - 127.0)
    codes = (blocks / scale).astype(np.float32).astype(dtype).astype(np.float64)
    return np.moveaxis((codes * scale).reshape(v.shape), -1, axis)


WIDE = False


def mx_kscale(k):
    if not WIDE:
        return np.ones(k)
    levels = np.array([10, -10, 5, -5, 0])
    a = np.random.permutation(np.resize(levels, k // 512 * 4)).reshape(k // 512, 4)
    idx = np.arange(k)
    return np.exp2(a[idx // 512, idx % 128 // 32])


BF16 = ml_dtypes.bfloat16


def bf(x):
    return np.asarray(x, np.float32).astype(BF16)


def f64(x):
    return np.asarray(x).astype(np.float64)


N, U0, U1, U2, F0, F1, F2, D1, D2 = 1024, 512, 256, 128, 1024, 512, 256, 3, 5


def silu(v):
    return v / (1.0 + np.exp(-v))


def norm_act(y, axis):
    n = np.sqrt(np.sum(y * y, axis=axis, keepdims=True))
    n_safe = np.where(n == 0, 1.0, n)
    return y * (silu(n) / n_safe)


def setup_inputs():
    s = mx_kscale(U0)
    x = np.random.standard_normal((N, U0 + U1 * D1))
    x[:, :U0] = x[:, :U0] * s
    return {"x": bf(x),
            "w1_l0": bf(np.random.standard_normal((U0, F0)) / s[:, None]),
            "w1_l1": bf(np.random.standard_normal((U1, F1))),
            "w2_l0": bf(np.random.standard_normal((F0, U0))),
            "w2_l1": bf(np.random.standard_normal((F1, U1)))}


def reference(x, w1_l0, w1_l1, w2_l0, w2_l1):
    x0 = f64(x)[:, :U0]
    y0 = (mxq(x0, 1, "e4m3") @ mxq(f64(w1_l0), 0, "e4m3")) * (1.0 / np.sqrt(U0))
    h0 = norm_act(y0[:, None, :], 1)[:, 0, :]
    o0 = (mxq(h0, 1, "e4m3") @ mxq(f64(w2_l0), 0, "e4m3")) * (1.0 / np.sqrt(F0))
    x1 = f64(x)[:, U0:].reshape(N, U1, D1).transpose(0, 2, 1)
    y1 = (x1 @ f64(w1_l1)) * (1.0 / np.sqrt(U1))
    h1 = norm_act(y1, 1)
    o1 = (mxq(h1, 2, "e4m3") @ mxq(f64(w2_l1), 0, "e4m3")) * (1.0 / np.sqrt(F1))
    return np.concatenate([o0, o1.transpose(0, 2, 1).reshape(N, U1 * D1)], axis=1)

@@ -1,0 +1,335 @@
+import math
+
+import concourse.mybir as mybir
+from concourse.masks import make_identity
+
+F32 = mybir.dt.float32
+BF16 = mybir.dt.bfloat16
+U32 = mybir.dt.uint32
+U8 = mybir.dt.uint8
+FP8X4 = mybir.dt.float8_e4m3fn_x4
+FUNC = mybir.ActivationFunctionType
+ALU = mybir.AluOpType
+
+P = 128
+PACK = 4
+ROWS = 1024
+TILES = ROWS // P
+U0, F0 = 512, 1024
+U1, F1, COMP = 256, 512, 3
+X_COLS = U0 + U1 * COMP
+K1 = U1 // P
+PASSES0 = F0 // (P * PACK)
+HALVES = U1 // P
+
+S_Y0 = 1.0 / math.sqrt(U0)
+S_O0 = 1.0 / math.sqrt(F0)
+S_Y1 = 1.0 / math.sqrt(U1)
+S_O1 = 1.0 / math.sqrt(F1)
+TINY = 1e-30
+
+FLOPS = 2 * ROWS * (U0 * F0 + F0 * U0 + COMP * U1 * F1 + COMP * F1 * U1)
+
+
+def tile_intermodule_pa_kernel(tc, x, w1_l0, w1_l1, w2_l0, w2_l1, out):
+    nc = tc.nc
+    with tc.tile_pool(name="keep", bufs=1) as keep, tc.tile_pool(name="two", bufs=2) as two, tc.tile_pool(
+        name="three", bufs=3
+    ) as three, tc.psum_pool(name="psum", bufs=1) as psum, tc.manual_schedule():
+
+        def bank(number, shape, dtype, name):
+            return psum.tile(shape, dtype, tag="bank%d" % number, name=name)
+
+        x_sb = [keep.tile([P, X_COLS], BF16, name="x_sb%d" % i) for i in range(TILES)]
+        w1l1_sb = keep.tile([P, K1, F1], BF16, name="w1l1_sb")
+        w1_raw = keep.tile([P, PACK, F0], BF16, name="w1_raw")
+        w2_raw = keep.tile([P, PASSES0 * PACK, U0], BF16, name="w2_raw")
+        v2_raw = keep.tile([P, PACK, U1], BF16, name="v2_raw")
+
+        def load_x(i):
+            nc.sync.dma_start(out=x_sb[i][:], in_=x[i * P : (i + 1) * P, :])
+
+        load_x(0)
+        nc.sync.dma_start(out=w1l1_sb[:], in_=w1_l1.rearrange("(k p) v -> p k v", p=P))
+        for u in range(2):
+            nc.sync.dma_start(
+                out=w1_raw[:, 2 * u : 2 * u + 2, :],
+                in_=w1_l0[256 * u : 256 * (u + 1), :].rearrange("(p e) f -> p e f", e=2),
+            )
+        for i in range(1, TILES):
+            load_x(i)
+        nc.sync.dma_start(out=v2_raw[:], in_=w2_l1.rearrange("(t p) w -> p t w", p=P))
+        nc.sync.dma_start(out=w2_raw[:], in_=w2_l0.rearrange("(a p) j -> p a j", p=P))
+
+        ident_f32 = keep.tile([P, P], F32, name="ident_f32")
+        ident_bf16 = keep.tile([P, P], BF16, name="ident_bf16")
+        make_identity(nc, ident_bf16[:])
+        make_identity(nc, ident_f32[:])
+
+        w1_grp = keep.tile([P, F0, PACK], BF16, name="w1_grp", align_bytes=64)
+        w1_codes = keep.tile([P, F0], U32, name="w1_codes", align_bytes=64)
+        w1_scales = keep.tile([P, F0], U8, name="w1_scales", align_bytes=64)
+        w2_grp = keep.tile([P, PASSES0, U0, PACK], BF16, name="w2_grp", align_bytes=64)
+        w2_codes = keep.tile([P, PASSES0, U0], U32, name="w2_codes", align_bytes=64)
+        w2_scales = keep.tile([P, PASSES0, U0], U8, name="w2_scales", align_bytes=64)
+        v2_grp = keep.tile([P, U1, PACK], BF16, name="v2_grp", align_bytes=64)
+        v2_codes = keep.tile([P, U1], U32, name="v2_codes", align_bytes=64)
+        v2_scales = keep.tile([P, U1], U8, name="v2_scales", align_bytes=64)
+        x0_codes = keep.tile([P, TILES, P], U32, name="x0_codes", align_bytes=64)
+        x0_scales = keep.tile([P, TILES, P], U8, name="x0_scales", align_bytes=64)
+        y1_sb = keep.tile([P, TILES, COMP, F1], F32, name="y1_sb")
+        gate1 = keep.tile([P, TILES, F1], F32, name="gate1")
+
+        def regroup(grouped, raw):
+            nc.vector.tensor_copy(
+                out=grouped.rearrange("p (c i) t -> p c t i", i=4),
+                in_=raw.rearrange("p t (c i) -> p c t i", i=4),
+            )
+
+        def quantise(codes, scales, grouped):
+            nc.vector.quantize_mx(out=codes.bitcast(FP8X4), scales=scales, in_=grouped)
+
+        x1t = {}
+        x0_grp = {}
+        y1_bank = {}
+        squares = {}
+
+        def transpose_x(i):
+            words = x_sb[i][:].bitcast(F32)
+            x0_ps = bank(0, [P, 2, P], F32, "x0_ps")
+            for u in range(2):
+                nc.tensor.transpose(x0_ps[:, u, :], words[:, u * P : (u + 1) * P], ident_f32[:])
+            x1_view = x_sb[i][:, U0:X_COLS].rearrange("p (k u c) -> p k c u", k=K1, u=P, c=COMP)
+            x1_ps = bank(1, [P, K1 * COMP, P], BF16, "x1_ps")
+            for k in range(K1):
+                for c in range(COMP):
+                    nc.tensor.transpose(x1_ps[:, k * COMP + c, :], x1_view[:, k, c, :], ident_bf16[:])
+            x0_grp[i] = three.tile([P, P * PACK], BF16, name="x0_grp", align_bytes=64)
+            nc.scalar.copy(
+                out=x0_grp[i][:].bitcast(F32).rearrange("p (n u) -> p n u", u=2),
+                in_=x0_ps[:].rearrange("p u n -> p n u"),
+            )
+            x1t[i] = three.tile([P, K1 * COMP, P], BF16, name="x1t")
+            nc.scalar.copy(out=x1t[i][:], in_=x1_ps[:])
+
+        def multiply_y1(i):
+            for c in range(COMP):
+                y1_bank[i, c] = bank(2 + COMP * (i % 2) + c, [P, PACK, P], F32, "y1_ps")
+                for t in range(PACK):
+                    for k in range(K1):
+                        nc.tensor.matmul(
+                            y1_bank[i, c][:, t, :],
+                            lhsT=w1l1_sb[:, k, t * P : (t + 1) * P],
+                            rhs=x1t[i][:, k * COMP + c, :],
+                            start=(k == 0),
+                            stop=(k == K1 - 1),
+                        )
+
+        def park_y1(i):
+            for c in range(COMP):
+                nc.vector.tensor_scalar(
+                    out=y1_sb[:, i, c, :].rearrange("p (n t) -> p n t", t=PACK),
+                    in0=y1_bank[i, c][:].rearrange("p t n -> p n t"),
+                    scalar1=S_Y1,
+                    scalar2=None,
+                    op0=ALU.mult,
+                )
+
+        def square_y1(i):
+            squares[i] = two.tile([P, COMP, F1], F32, name="squares")
+            nc.scalar.activation(out=squares[i][:], in_=y1_sb[:, i, :, :], func=FUNC.Square)
+
+        def add_squares_first(i):
+            nc.vector.tensor_tensor(
+                out=gate1[:, i, :], in0=squares[i][:, 0, :], in1=squares[i][:, 1, :], op=ALU.add
+            )
+
+        def add_squares_last(i):
+            nc.vector.scalar_tensor_tensor(
+                out=gate1[:, i, :],
+                in0=gate1[:, i, :],
+                scalar=TINY,
+                in1=squares[i][:, 2, :],
+                op0=ALU.max,
+                op1=ALU.add,
+            )
+
+        def root(i):
+            nc.scalar.activation(out=gate1[:, i, :], in_=gate1[:, i, :], func=FUNC.Sqrt)
+
+        def quantise_x0(i):
+            quantise(x0_codes[:, i, :], x0_scales[:, i, :], x0_grp[i][:])
+
+        y0_bank = {}
+        gate0 = {}
+        h0_codes = {}
+        h0_scales = {}
+        h1_codes = {}
+        h1_scales = {}
+        h0_grp = {}
+        h1_grp = {}
+        o0_bank = {}
+        o1_bank = {}
+        staged = {}
+
+        def multiply_y0(i):
+            for g in range(PASSES0):
+                y0_bank[i, g] = bank(PASSES0 * (i % 2) + g, [P, PACK, P], F32, "y0_ps")
+                for t in range(PACK):
+                    cols = slice((g * PACK + t) * P, (g * PACK + t + 1) * P)
+                    nc.tensor.matmul_mx(
+                        out=y0_bank[i, g][:, t, :],
+                        lhsT=w1_codes[:, cols].bitcast(FP8X4),
+                        lhsT_scale=w1_scales[:, cols],
+                        rhs=x0_codes[:, i, :].bitcast(FP8X4),
+                        rhs_scale=x0_scales[:, i, :],
+                        start=True,
+                        stop=True,
+                    )
+
+        def abs_y0(i):
+            gate0[i] = two.tile([P, PASSES0, F1], F32, name="gate0")
+            for g in range(PASSES0):
+                nc.scalar.activation(
+                    out=gate0[i][:, g, :].rearrange("p (n t) -> p n t", t=PACK),
+                    in_=y0_bank[i, g][:].rearrange("p t n -> p n t"),
+                    func=FUNC.Abs,
+                    scale=S_Y0,
+                )
+
+        def sigmoids(i):
+            nc.scalar.activation(out=gate0[i][:], in_=gate0[i][:], func=FUNC.Sigmoid)
+            nc.scalar.activation(out=gate1[:, i, :], in_=gate1[:, i, :], func=FUNC.Sigmoid)
+
+        def gate_y1(i):
+            h1_grp[i] = two.tile([P, COMP, F1], BF16, name="h1_grp", align_bytes=64)
+            nc.vector.tensor_tensor(
+                out=h1_grp[i][:],
+                in0=y1_sb[:, i, :, :],
+                in1=gate1[:, i, :].unsqueeze(1).to_broadcast([P, COMP, F1]),
+                op=ALU.mult,
+            )
+            h1_codes[i] = two.tile([P, COMP, P], U32, name="h1_codes", align_bytes=64)
+            h1_scales[i] = two.tile([P, COMP, P], U8, name="h1_scales", align_bytes=64)
+
+        def gate_y0(i, g):
+            if g == 0:
+                h0_grp[i] = two.tile([P, PASSES0, F1], BF16, name="h0_grp", align_bytes=64)
+            nc.vector.scalar_tensor_tensor(
+                out=h0_grp[i][:, g, :].rearrange("p (n t) -> p n t", t=PACK),
+                in0=y0_bank[i, g][:].rearrange("p t n -> p n t"),
+                scalar=S_Y0,
+                in1=gate0[i][:, g, :].rearrange("p (n t) -> p n t", t=PACK),
+                op0=ALU.mult,
+                op1=ALU.mult,
+            )
+
+        def quantise_h1(i, first, count):
+            quantise(
+                h1_codes[i][:, first : first + count, :].rearrange("p c n -> p (c n)"),
+                h1_scales[i][:, first : first + count, :].rearrange("p c n -> p (c n)"),
+                h1_grp[i][:, first : first + count, :].rearrange("p c f -> p (c f)"),
+            )
+
+        def quantise_h0(i):
+            h0_codes[i] = two.tile([P, PASSES0, P], U32, name="h0_codes", align_bytes=64)
+            h0_scales[i] = two.tile([P, PASSES0, P], U8, name="h0_scales", align_bytes=64)
+            quantise(
+                h0_codes[i][:].rearrange("p g n -> p (g n)"),
+                h0_scales[i][:].rearrange("p g n -> p (g n)"),
+                h0_grp[i][:].rearrange("p g f -> p (g f)"),
+            )
+
+        def multiply_o1(i):
+            for h in range(HALVES):
+                o1_bank[i, h] = bank(6 + h, [P, COMP, P], F32, "o1_ps")
+                for c in range(COMP):
+                    nc.tensor.matmul_mx(
+                        out=o1_bank[i, h][:, c, :],
+                        lhsT=h1_codes[i][:, c, :].bitcast(FP8X4),
+                        lhsT_scale=h1_scales[i][:, c, :],
+                        rhs=v2_codes[:, h * P : (h + 1) * P].bitcast(FP8X4),
+                        rhs_scale=v2_scales[:, h * P : (h + 1) * P],
+                        start=True,
+                        stop=True,
+                    )
+
+        def multiply_o0(i):
+            o0_bank[i] = bank(4 + i % 2, [P, U0], F32, "o0_ps")
+            for g in range(PASSES0):
+                nc.tensor.matmul_mx(
+                    out=o0_bank[i][:],
+                    lhsT=h0_codes[i][:, g, :].bitcast(FP8X4),
+                    lhsT_scale=h0_scales[i][:, g, :],
+                    rhs=w2_codes[:, g, :].bitcast(FP8X4),
+                    rhs_scale=w2_scales[:, g, :],
+                    start=(g == 0),
+                    stop=(g == PASSES0 - 1),
+                )
+
+        def store(i):
+            staged[i] = three.tile([P, X_COLS], F32, name="staged")
+            for h in range(HALVES):
+                first = U0 + h * P * COMP
+                nc.scalar.activation(
+                    out=staged[i][:, first : first + P * COMP].rearrange("p (w c) -> p w c", c=COMP),
+                    in_=o1_bank[i, h][:].rearrange("p c w -> p w c"),
+                    func=FUNC.Copy,
+                    scale=S_O1,
+                )
+            nc.scalar.activation(out=staged[i][:, 0:U0], in_=o0_bank[i][:], func=FUNC.Copy, scale=S_O0)
+            nc.sync.dma_start(out=out[i * P : (i + 1) * P, :], in_=staged[i][:])
+
+        transpose_x(0)
+        half = F0 // 2
+        for a in range(2):
+            regroup(w1_grp[:, a * half : (a + 1) * half, :], w1_raw[:, :, a * half : (a + 1) * half])
+        for a in range(2):
+            cols = slice(a * half, (a + 1) * half)
+            quantise(w1_codes[:, cols], w1_scales[:, cols], w1_grp[:, cols, :].rearrange("p w t -> p (w t)"))
+
+        for i in range(TILES):
+            multiply_y1(i)
+            for j in ([1, 2] if i == 0 else [i + 2]):
+                if j < TILES:
+                    transpose_x(j)
+            park_y1(i)
+            if i > 0:
+                add_squares_first(i - 1)
+            quantise_x0(i)
+            if i > 0:
+                add_squares_last(i - 1)
+            square_y1(i)
+            if i > 0:
+                root(i - 1)
+
+        last = TILES - 1
+        multiply_y0(0)
+        multiply_y0(1)
+        abs_y0(0)
+        add_squares_first(last)
+        regroup(v2_grp[:], v2_raw[:])
+        add_squares_last(last)
+        root(last)
+        for g in range(PASSES0):
+            regroup(w2_grp[:, g, :, :], w2_raw[:, g * PACK : (g + 1) * PACK, :])
+        quantise(v2_codes[:], v2_scales[:], v2_grp[:].rearrange("p w t -> p (w t)"))
+        for g in range(PASSES0):
+            quantise(w2_codes[:, g, :], w2_scales[:, g, :], w2_grp[:, g, :, :].rearrange("p w t -> p (w t)"))
+        sigmoids(0)
+
+        for i in range(TILES):
+            if i + 1 < TILES:
+                abs_y0(i + 1)
+                sigmoids(i + 1)
+            gate_y1(i)
+            gate_y0(i, 0)
+            quantise_h1(i, 0, 2)
+            gate_y0(i, 1)
+            quantise_h1(i, 2, 1)
+            quantise_h0(i)
+            if i + 2 < TILES:
+                multiply_y0(i + 2)
+            multiply_o1(i)
+            multiply_o0(i)
+            store(i)

@@ -51,12 +51,14 @@ def tile_intermodule_pa_kernel(tc, x, w1_l0, w1_l1, w2_l0, w2_l1, out):
 
         load_x(0)
         nc.sync.dma_start(out=w1l1_sb[:], in_=w1_l1.rearrange("(k p) v -> p k v", p=P))
+        load_x(1)
+        load_x(2)
         for u in range(2):
             nc.sync.dma_start(
                 out=w1_raw[:, 2 * u : 2 * u + 2, :],
                 in_=w1_l0[256 * u : 256 * (u + 1), :].rearrange("(p e) f -> p e f", e=2),
             )
-        for i in range(1, TILES):
+        for i in range(3, TILES):
             load_x(i)
         nc.sync.dma_start(out=v2_raw[:], in_=w2_l1.rearrange("(t p) w -> p t w", p=P))
         nc.sync.dma_start(out=w2_raw[:], in_=w2_l0.rearrange("(a p) j -> p a j", p=P))
@@ -65,6 +67,8 @@ def tile_intermodule_pa_kernel(tc, x, w1_l0, w1_l1, w2_l0, w2_l1, out):
         ident_bf16 = keep.tile([P, P], BF16, name="ident_bf16")
         make_identity(nc, ident_bf16[:])
         make_identity(nc, ident_f32[:])
+        tiny = keep.tile([P, 1], F32, name="tiny")
+        nc.vector.memset(tiny[:], TINY)
 
         w1_grp = keep.tile([P, F0, PACK], BF16, name="w1_grp", align_bytes=64)
         w1_codes = keep.tile([P, F0], U32, name="w1_codes", align_bytes=64)
@@ -75,6 +79,7 @@ def tile_intermodule_pa_kernel(tc, x, w1_l0, w1_l1, w2_l0, w2_l1, out):
         v2_grp = keep.tile([P, U1, PACK], BF16, name="v2_grp", align_bytes=64)
         v2_codes = keep.tile([P, U1], U32, name="v2_codes", align_bytes=64)
         v2_scales = keep.tile([P, U1], U8, name="v2_scales", align_bytes=64)
+        x0_grp = keep.tile([P, TILES, P * PACK], BF16, name="x0_grp", align_bytes=64)
         x0_codes = keep.tile([P, TILES, P], U32, name="x0_codes", align_bytes=64)
         x0_scales = keep.tile([P, TILES, P], U8, name="x0_scales", align_bytes=64)
         y1_sb = keep.tile([P, TILES, COMP, F1], F32, name="y1_sb")
@@ -89,28 +94,30 @@ def tile_intermodule_pa_kernel(tc, x, w1_l0, w1_l1, w2_l0, w2_l1, out):
         def quantise(codes, scales, grouped):
             nc.vector.quantize_mx(out=codes.bitcast(FP8X4), scales=scales, in_=grouped)
 
+        x0_ps = {}
+        x1_ps = {}
         x1t = {}
-        x0_grp = {}
         y1_bank = {}
         squares = {}
 
         def transpose_x(i):
-            words = x_sb[i][:].bitcast(F32)
-            x0_ps = bank(0, [P, 2, P], F32, "x0_ps")
-            for u in range(2):
-                nc.tensor.transpose(x0_ps[:, u, :], words[:, u * P : (u + 1) * P], ident_f32[:])
             x1_view = x_sb[i][:, U0:X_COLS].rearrange("p (k u c) -> p k c u", k=K1, u=P, c=COMP)
-            x1_ps = bank(1, [P, K1 * COMP, P], BF16, "x1_ps")
+            x1_ps[i] = bank(1, [P, K1 * COMP, P], BF16, "x1_ps")
             for k in range(K1):
                 for c in range(COMP):
-                    nc.tensor.transpose(x1_ps[:, k * COMP + c, :], x1_view[:, k, c, :], ident_bf16[:])
-            x0_grp[i] = three.tile([P, P * PACK], BF16, name="x0_grp", align_bytes=64)
-            nc.scalar.copy(
-                out=x0_grp[i][:].bitcast(F32).rearrange("p (n u) -> p n u", u=2),
-                in_=x0_ps[:].rearrange("p u n -> p n u"),
-            )
+                    nc.tensor.transpose(x1_ps[i][:, k * COMP + c, :], x1_view[:, k, c, :], ident_bf16[:])
+            words = x_sb[i][:].bitcast(F32)
+            x0_ps[i] = bank(0, [P, 2, P], F32, "x0_ps")
+            for u in range(2):
+                nc.tensor.transpose(x0_ps[i][:, u, :], words[:, u * P : (u + 1) * P], ident_f32[:])
+
+        def copy_x(i):
             x1t[i] = three.tile([P, K1 * COMP, P], BF16, name="x1t")
-            nc.scalar.copy(out=x1t[i][:], in_=x1_ps[:])
+            nc.scalar.copy(out=x1t[i][:], in_=x1_ps[i][:])
+            nc.vector.tensor_copy(
+                out=x0_grp[:, i, :].bitcast(F32).rearrange("p (n u) -> p n u", u=2),
+                in_=x0_ps[i][:].rearrange("p u n -> p n u"),
+            )
 
         def multiply_y1(i):
             for c in range(COMP):
@@ -136,29 +143,25 @@ def tile_intermodule_pa_kernel(tc, x, w1_l0, w1_l1, w2_l0, w2_l1, out):
                 )
 
         def square_y1(i):
-            squares[i] = two.tile([P, COMP, F1], F32, name="squares")
-            nc.scalar.activation(out=squares[i][:], in_=y1_sb[:, i, :, :], func=FUNC.Square)
+            squares[i] = three.tile([P, COMP, F1], F32, name="squares")
+            for c in range(COMP):
+                nc.scalar.activation(out=squares[i][:, c, :], in_=y1_sb[:, i, c, :], func=FUNC.Square)
 
-        def add_squares_first(i):
-            nc.vector.tensor_tensor(
+        def add_squares(i):
+            nc.gpsimd.tensor_tensor(
                 out=gate1[:, i, :], in0=squares[i][:, 0, :], in1=squares[i][:, 1, :], op=ALU.add
             )
-
-        def add_squares_last(i):
-            nc.vector.scalar_tensor_tensor(
-                out=gate1[:, i, :],
-                in0=gate1[:, i, :],
-                scalar=TINY,
-                in1=squares[i][:, 2, :],
-                op0=ALU.max,
-                op1=ALU.add,
-            )
+            nc.gpsimd.tensor_tensor(out=gate1[:, i, :], in0=gate1[:, i, :], in1=squares[i][:, 2, :], op=ALU.add)
 
         def root(i):
-            nc.scalar.activation(out=gate1[:, i, :], in_=gate1[:, i, :], func=FUNC.Sqrt)
+            nc.scalar.activation(out=gate1[:, i, :], in_=gate1[:, i, :], func=FUNC.Sqrt, bias=tiny[:])
 
-        def quantise_x0(i):
-            quantise(x0_codes[:, i, :], x0_scales[:, i, :], x0_grp[i][:])
+        def quantise_x0(first, count):
+            quantise(
+                x0_codes[:, first : first + count, :].rearrange("p i n -> p (i n)"),
+                x0_scales[:, first : first + count, :].rearrange("p i n -> p (i n)"),
+                x0_grp[:, first : first + count, :].rearrange("p i f -> p (i f)"),
+            )
 
         y0_bank = {}
         gate0 = {}
@@ -198,8 +201,8 @@ def tile_intermodule_pa_kernel(tc, x, w1_l0, w1_l1, w2_l0, w2_l1, out):
                 )
 
         def sigmoids(i):
-            nc.scalar.activation(out=gate0[i][:], in_=gate0[i][:], func=FUNC.Sigmoid)
             nc.scalar.activation(out=gate1[:, i, :], in_=gate1[:, i, :], func=FUNC.Sigmoid)
+            nc.scalar.activation(out=gate0[i][:], in_=gate0[i][:], func=FUNC.Sigmoid)
 
         def gate_y1(i):
             h1_grp[i] = two.tile([P, COMP, F1], BF16, name="h1_grp", align_bytes=64)
@@ -267,61 +270,77 @@ def tile_intermodule_pa_kernel(tc, x, w1_l0, w1_l1, w2_l0, w2_l1, out):
                     stop=(g == PASSES0 - 1),
                 )
 
-        def store(i):
-            staged[i] = three.tile([P, X_COLS], F32, name="staged")
-            for h in range(HALVES):
-                first = U0 + h * P * COMP
-                nc.scalar.activation(
-                    out=staged[i][:, first : first + P * COMP].rearrange("p (w c) -> p w c", c=COMP),
-                    in_=o1_bank[i, h][:].rearrange("p c w -> p w c"),
-                    func=FUNC.Copy,
-                    scale=S_O1,
-                )
-            nc.scalar.activation(out=staged[i][:, 0:U0], in_=o0_bank[i][:], func=FUNC.Copy, scale=S_O0)
-            nc.sync.dma_start(out=out[i * P : (i + 1) * P, :], in_=staged[i][:])
+        def o1_views(i, h):
+            first = U0 + h * P * COMP
+            return (
+                staged[i][:, first : first + P * COMP].rearrange("p (w c) -> p w c", c=COMP),
+                o1_bank[i, h][:].rearrange("p c w -> p w c"),
+            )
 
-        transpose_x(0)
+        def finish_on_scalar(i):
+            staged[i] = three.tile([P, X_COLS], F32, name="staged")
+            to_sbuf, from_psum = o1_views(i, 0)
+            nc.scalar.activation(out=to_sbuf, in_=from_psum, func=FUNC.Copy, scale=S_O1)
+            nc.scalar.activation(out=staged[i][:, 0:U0], in_=o0_bank[i][:], func=FUNC.Copy, scale=S_O0)
+            nc.sync.dma_start(out=out[i * P : (i + 1) * P, 0:U0], in_=staged[i][:, 0:U0])
+
+        def finish_on_vector(i):
+            to_sbuf, from_psum = o1_views(i, 1)
+            nc.vector.tensor_scalar(out=to_sbuf, in0=from_psum, scalar1=S_O1, scalar2=None, op0=ALU.mult)
+            nc.sync.dma_start(out=out[i * P : (i + 1) * P, U0:X_COLS], in_=staged[i][:, U0:X_COLS])
+
         half = F0 // 2
-        for a in range(2):
+
+        def regroup_w1(a):
             regroup(w1_grp[:, a * half : (a + 1) * half, :], w1_raw[:, :, a * half : (a + 1) * half])
-        for a in range(2):
+
+        def quantise_w1(a):
             cols = slice(a * half, (a + 1) * half)
             quantise(w1_codes[:, cols], w1_scales[:, cols], w1_grp[:, cols, :].rearrange("p w t -> p (w t)"))
 
+        preparation = [
+            lambda: regroup_w1(0),
+            lambda: regroup_w1(1),
+            lambda: quantise_w1(0),
+            lambda: quantise_w1(1),
+            lambda: quantise_x0(0, TILES // 2),
+            lambda: regroup(v2_grp[:], v2_raw[:]),
+            lambda: quantise_x0(TILES // 2, TILES // 2),
+            lambda: quantise(v2_codes[:], v2_scales[:], v2_grp[:].rearrange("p w t -> p (w t)")),
+        ]
+
+        for i in range(2):
+            transpose_x(i)
+            copy_x(i)
         for i in range(TILES):
             multiply_y1(i)
-            for j in ([1, 2] if i == 0 else [i + 2]):
-                if j < TILES:
-                    transpose_x(j)
+            if i + 2 < TILES:
+                transpose_x(i + 2)
             park_y1(i)
-            if i > 0:
-                add_squares_first(i - 1)
-            quantise_x0(i)
-            if i > 0:
-                add_squares_last(i - 1)
             square_y1(i)
-            if i > 0:
-                root(i - 1)
+            add_squares(i)
+            if i + 2 < TILES:
+                copy_x(i + 2)
+            preparation[i]()
+            if i >= 2:
+                root(i - 2)
 
-        last = TILES - 1
-        multiply_y0(0)
-        multiply_y0(1)
-        abs_y0(0)
-        add_squares_first(last)
-        regroup(v2_grp[:], v2_raw[:])
-        add_squares_last(last)
-        root(last)
+        for i in range(2):
+            multiply_y0(i)
+        for i in range(2):
+            abs_y0(i)
+            root(TILES - 2 + i)
         for g in range(PASSES0):
             regroup(w2_grp[:, g, :, :], w2_raw[:, g * PACK : (g + 1) * PACK, :])
-        quantise(v2_codes[:], v2_scales[:], v2_grp[:].rearrange("p w t -> p (w t)"))
         for g in range(PASSES0):
             quantise(w2_codes[:, g, :], w2_scales[:, g, :], w2_grp[:, g, :, :].rearrange("p w t -> p (w t)"))
         sigmoids(0)
 
         for i in range(TILES):
             if i + 1 < TILES:
-                abs_y0(i + 1)
                 sigmoids(i + 1)
+            if i > 0:
+                finish_on_vector(i - 1)
             gate_y1(i)
             gate_y0(i, 0)
             quantise_h1(i, 0, 2)
@@ -332,4 +351,7 @@ def tile_intermodule_pa_kernel(tc, x, w1_l0, w1_l1, w2_l0, w2_l1, out):
                 multiply_y0(i + 2)
             multiply_o1(i)
             multiply_o0(i)
-            store(i)
+            finish_on_scalar(i)
+            if i + 2 < TILES:
+                abs_y0(i + 2)
+        finish_on_vector(TILES - 1)

@@ -340,8 +340,10 @@ def tile_intermodule_pa_kernel(tc, x, w1_l0, w1_l1, w2_l0, w2_l1, out):
             if i + 1 < TILES:
                 sigmoids(i + 1)
             if i > 0:
-                finish_on_vector(i - 1)
+                finish_on_scalar(i - 1)
             gate_y1(i)
+            if i > 0:
+                finish_on_vector(i - 1)
             gate_y0(i, 0)
             quantise_h1(i, 0, 2)
             gate_y0(i, 1)
@@ -349,9 +351,8 @@ def tile_intermodule_pa_kernel(tc, x, w1_l0, w1_l1, w2_l0, w2_l1, out):
             quantise_h0(i)
             if i + 2 < TILES:
                 multiply_y0(i + 2)
+                abs_y0(i + 2)
             multiply_o1(i)
             multiply_o0(i)
-            finish_on_scalar(i)
-            if i + 2 < TILES:
-                abs_y0(i + 2)
+        finish_on_scalar(TILES - 1)
         finish_on_vector(TILES - 1)

@@ -114,7 +114,7 @@ def tile_intermodule_pa_kernel(tc, x, w1_l0, w1_l1, w2_l0, w2_l1, out):
         def copy_x(i):
             x1t[i] = three.tile([P, K1 * COMP, P], BF16, name="x1t")
             nc.scalar.copy(out=x1t[i][:], in_=x1_ps[i][:])
-            nc.vector.tensor_copy(
+            nc.scalar.copy(
                 out=x0_grp[:, i, :].bitcast(F32).rearrange("p (n u) -> p n u", u=2),
                 in_=x0_ps[i][:].rearrange("p u n -> p n u"),
             )
@@ -147,11 +147,13 @@ def tile_intermodule_pa_kernel(tc, x, w1_l0, w1_l1, w2_l0, w2_l1, out):
             for c in range(COMP):
                 nc.scalar.activation(out=squares[i][:, c, :], in_=y1_sb[:, i, c, :], func=FUNC.Square)
 
-        def add_squares(i):
-            nc.gpsimd.tensor_tensor(
+        def add_squares_first(i):
+            nc.vector.tensor_tensor(
                 out=gate1[:, i, :], in0=squares[i][:, 0, :], in1=squares[i][:, 1, :], op=ALU.add
             )
-            nc.gpsimd.tensor_tensor(out=gate1[:, i, :], in0=gate1[:, i, :], in1=squares[i][:, 2, :], op=ALU.add)
+
+        def add_squares_last(i):
+            nc.vector.tensor_tensor(out=gate1[:, i, :], in0=gate1[:, i, :], in1=squares[i][:, 2, :], op=ALU.add)
 
         def root(i):
             nc.scalar.activation(out=gate1[:, i, :], in_=gate1[:, i, :], func=FUNC.Sqrt, bias=tiny[:])
@@ -318,13 +320,18 @@ def tile_intermodule_pa_kernel(tc, x, w1_l0, w1_l1, w2_l0, w2_l1, out):
                 transpose_x(i + 2)
             park_y1(i)
             square_y1(i)
-            add_squares(i)
             if i + 2 < TILES:
                 copy_x(i + 2)
+            if i >= 1:
+                add_squares_first(i - 1)
             preparation[i]()
+            if i >= 1:
+                add_squares_last(i - 1)
             if i >= 2:
                 root(i - 2)
 
+        add_squares_first(TILES - 1)
+        add_squares_last(TILES - 1)
         for i in range(2):
             multiply_y0(i)
         for i in range(2):

@@ -52,6 +52,7 @@ def tile_intermodule_pa_kernel(tc, x, w1_l0, w1_l1, w2_l0, w2_l1, out):
         load_x(0)
         nc.sync.dma_start(out=w1l1_sb[:], in_=w1_l1.rearrange("(k p) v -> p k v", p=P))
         load_x(1)
+        nc.sync.dma_start(out=v2_raw[:], in_=w2_l1.rearrange("(t p) w -> p t w", p=P))
         load_x(2)
         for u in range(2):
             nc.sync.dma_start(
@@ -60,7 +61,6 @@ def tile_intermodule_pa_kernel(tc, x, w1_l0, w1_l1, w2_l0, w2_l1, out):
             )
         for i in range(3, TILES):
             load_x(i)
-        nc.sync.dma_start(out=v2_raw[:], in_=w2_l1.rearrange("(t p) w -> p t w", p=P))
         nc.sync.dma_start(out=w2_raw[:], in_=w2_l0.rearrange("(a p) j -> p a j", p=P))
 
         ident_f32 = keep.tile([P, P], F32, name="ident_f32")
@@ -114,7 +114,7 @@ def tile_intermodule_pa_kernel(tc, x, w1_l0, w1_l1, w2_l0, w2_l1, out):
         def copy_x(i):
             x1t[i] = three.tile([P, K1 * COMP, P], BF16, name="x1t")
             nc.scalar.copy(out=x1t[i][:], in_=x1_ps[i][:])
-            nc.scalar.copy(
+            nc.vector.tensor_copy(
                 out=x0_grp[:, i, :].bitcast(F32).rearrange("p (n u) -> p n u", u=2),
                 in_=x0_ps[i][:].rearrange("p u n -> p n u"),
             )
@@ -134,18 +134,16 @@ def tile_intermodule_pa_kernel(tc, x, w1_l0, w1_l1, w2_l0, w2_l1, out):
 
         def park_y1(i):
             for c in range(COMP):
-                nc.vector.tensor_scalar(
-                    out=y1_sb[:, i, c, :].rearrange("p (n t) -> p n t", t=PACK),
-                    in0=y1_bank[i, c][:].rearrange("p t n -> p n t"),
-                    scalar1=S_Y1,
-                    scalar2=None,
-                    op0=ALU.mult,
-                )
+                to_sbuf = y1_sb[:, i, c, :].rearrange("p (n t) -> p n t", t=PACK)
+                from_psum = y1_bank[i, c][:].rearrange("p t n -> p n t")
+                if c == 0:
+                    nc.scalar.activation(out=to_sbuf, in_=from_psum, func=FUNC.Copy, scale=S_Y1)
+                else:
+                    nc.vector.tensor_scalar(out=to_sbuf, in0=from_psum, scalar1=S_Y1, scalar2=None, op0=ALU.mult)
 
         def square_y1(i):
             squares[i] = three.tile([P, COMP, F1], F32, name="squares")
-            for c in range(COMP):
-                nc.scalar.activation(out=squares[i][:, c, :], in_=y1_sb[:, i, c, :], func=FUNC.Square)
+            nc.scalar.activation(out=squares[i][:], in_=y1_sb[:, i, :, :], func=FUNC.Square)
 
         def add_squares_first(i):
             nc.vector.tensor_tensor(
@@ -306,10 +304,11 @@ def tile_intermodule_pa_kernel(tc, x, w1_l0, w1_l1, w2_l0, w2_l1, out):
             lambda: quantise_w1(0),
             lambda: quantise_w1(1),
             lambda: quantise_x0(0, TILES // 2),
-            lambda: regroup(v2_grp[:], v2_raw[:]),
             lambda: quantise_x0(TILES // 2, TILES // 2),
-            lambda: quantise(v2_codes[:], v2_scales[:], v2_grp[:].rearrange("p w t -> p (w t)")),
         ]
+
+        regroup(v2_grp[:], v2_raw[:])
+        quantise(v2_codes[:], v2_scales[:], v2_grp[:].rearrange("p w t -> p (w t)"))
 
         for i in range(2):
             transpose_x(i)
@@ -319,29 +318,31 @@ def tile_intermodule_pa_kernel(tc, x, w1_l0, w1_l1, w2_l0, w2_l1, out):
             if i + 2 < TILES:
                 transpose_x(i + 2)
             park_y1(i)
-            square_y1(i)
             if i + 2 < TILES:
                 copy_x(i + 2)
             if i >= 1:
                 add_squares_first(i - 1)
-            preparation[i]()
+            if i < len(preparation):
+                preparation[i]()
             if i >= 1:
                 add_squares_last(i - 1)
             if i >= 2:
                 root(i - 2)
+            square_y1(i)
 
         add_squares_first(TILES - 1)
         add_squares_last(TILES - 1)
         for i in range(2):
             multiply_y0(i)
-        for i in range(2):
-            abs_y0(i)
-            root(TILES - 2 + i)
+        abs_y0(0)
+        for i in range(TILES - 2, TILES):
+            root(i)
         for g in range(PASSES0):
             regroup(w2_grp[:, g, :, :], w2_raw[:, g * PACK : (g + 1) * PACK, :])
         for g in range(PASSES0):
             quantise(w2_codes[:, g, :], w2_scales[:, g, :], w2_grp[:, g, :, :].rearrange("p w t -> p (w t)"))
         sigmoids(0)
+        abs_y0(1)
 
         for i in range(TILES):
             if i + 1 < TILES:

@@ -26,6 +26,15 @@ S_Y0 = 1.0 / math.sqrt(U0)
 S_O0 = 1.0 / math.sqrt(F0)
 S_Y1 = 1.0 / math.sqrt(U1)
 S_O1 = 1.0 / math.sqrt(F1)
+PARKED = [0, 1, 2, 3]
+AGAIN = [4, 5]
+KEPT = [6, 7]
+TENSOR_SUMS = [6, 7]
+PIECE = 64
+VECTOR_COPIES = [1, 2]
+LATE_ROOTS = [4, 5]
+SCALAR_PARKS = [0, 1, 2, 3]
+WARM_UP = 18
 TINY = 1e-30
 
 FLOPS = 2 * ROWS * (U0 * F0 + F0 * U0 + COMP * U1 * F1 + COMP * F1 * U1)
@@ -46,29 +55,38 @@ def tile_intermodule_pa_kernel(tc, x, w1_l0, w1_l1, w2_l0, w2_l1, out):
         w2_raw = keep.tile([P, PASSES0 * PACK, U0], BF16, name="w2_raw")
         v2_raw = keep.tile([P, PACK, U1], BF16, name="v2_raw")
 
-        def load_x(i):
-            nc.sync.dma_start(out=x_sb[i][:], in_=x[i * P : (i + 1) * P, :])
+        def load_x(i, first=0, end=X_COLS):
+            nc.sync.dma_start(out=x_sb[i][:, first:end], in_=x[i * P : (i + 1) * P, first:end])
 
-        load_x(0)
+        def load_w1(first, end):
+            for u in range(2):
+                nc.sync.dma_start(
+                    out=w1_raw[:, 2 * u : 2 * u + 2, first:end],
+                    in_=w1_l0[256 * u : 256 * (u + 1), first:end].rearrange("(p e) f -> p e f", e=2),
+                )
+
+        load_x(0, U0, X_COLS)
         nc.sync.dma_start(out=w1l1_sb[:], in_=w1_l1.rearrange("(k p) v -> p k v", p=P))
-        load_x(1)
         nc.sync.dma_start(out=v2_raw[:], in_=w2_l1.rearrange("(t p) w -> p t w", p=P))
+        load_x(1)
+        load_x(0, 0, U0)
         load_x(2)
-        for u in range(2):
-            nc.sync.dma_start(
-                out=w1_raw[:, 2 * u : 2 * u + 2, :],
-                in_=w1_l0[256 * u : 256 * (u + 1), :].rearrange("(p e) f -> p e f", e=2),
-            )
-        for i in range(3, TILES):
+        load_w1(0, F0 // 2)
+        load_x(3)
+        load_w1(F0 // 2, F0)
+        for i in range(4, TILES):
             load_x(i)
         nc.sync.dma_start(out=w2_raw[:], in_=w2_l0.rearrange("(a p) j -> p a j", p=P))
+
+        tiny = keep.tile([P, 1], F32, name="tiny")
+        nc.vector.memset(tiny[:], TINY)
+        first_root = keep.tile([P, 1], F32, name="first_root")
+        nc.scalar.activation(out=first_root[:], in_=tiny[:], func=FUNC.Sqrt)
 
         ident_f32 = keep.tile([P, P], F32, name="ident_f32")
         ident_bf16 = keep.tile([P, P], BF16, name="ident_bf16")
         make_identity(nc, ident_bf16[:])
         make_identity(nc, ident_f32[:])
-        tiny = keep.tile([P, 1], F32, name="tiny")
-        nc.vector.memset(tiny[:], TINY)
 
         w1_grp = keep.tile([P, F0, PACK], BF16, name="w1_grp", align_bytes=64)
         w1_codes = keep.tile([P, F0], U32, name="w1_codes", align_bytes=64)
@@ -82,68 +100,121 @@ def tile_intermodule_pa_kernel(tc, x, w1_l0, w1_l1, w2_l0, w2_l1, out):
         x0_grp = keep.tile([P, TILES, P * PACK], BF16, name="x0_grp", align_bytes=64)
         x0_codes = keep.tile([P, TILES, P], U32, name="x0_codes", align_bytes=64)
         x0_scales = keep.tile([P, TILES, P], U8, name="x0_scales", align_bytes=64)
-        y1_sb = keep.tile([P, TILES, COMP, F1], F32, name="y1_sb")
+        y1_sb = keep.tile([P, len(PARKED), COMP, F1], F32, name="y1_sb")
         gate1 = keep.tile([P, TILES, F1], F32, name="gate1")
 
-        def regroup(grouped, raw):
-            nc.vector.tensor_copy(
-                out=grouped.rearrange("p (c i) t -> p c t i", i=4),
-                in_=raw.rearrange("p t (c i) -> p c t i", i=4),
-            )
+        def regroup(grouped, raw, on_gpsimd=False):
+            if on_gpsimd:
+                nc.gpsimd.tensor_scalar(
+                    out=grouped, in0=raw.rearrange("p t w -> p w t"), scalar1=1.0, scalar2=0.0, op0=ALU.mult, op1=ALU.add
+                )
+            else:
+                nc.vector.tensor_copy(
+                    out=grouped.rearrange("p (c i) t -> p c t i", i=4),
+                    in_=raw.rearrange("p t (c i) -> p c t i", i=4),
+                )
 
         def quantise(codes, scales, grouped):
             nc.vector.quantize_mx(out=codes.bitcast(FP8X4), scales=scales, in_=grouped)
+
+        warm_in = keep.tile([P, P * PACK], BF16, name="warm_in", align_bytes=64)
+        warm_codes = keep.tile([P, P], U32, name="warm_codes", align_bytes=64)
+        warm_scales = keep.tile([P, P], U8, name="warm_scales", align_bytes=64)
+        nc.vector.memset(warm_in[:], 0.0)
+        quantise(warm_codes[:], warm_scales[:], warm_in[:])
+        warm_ps = bank(7, [P, PACK, P], F32, "warm_ps")
+        for i in range(WARM_UP):
+            nc.tensor.matmul_mx(
+                out=warm_ps[:, i % PACK, :],
+                lhsT=warm_codes[:].bitcast(FP8X4),
+                lhsT_scale=warm_scales[:],
+                rhs=warm_codes[:].bitcast(FP8X4),
+                rhs_scale=warm_scales[:],
+                start=True,
+                stop=True,
+            )
 
         x0_ps = {}
         x1_ps = {}
         x1t = {}
         y1_bank = {}
         squares = {}
+        sums = {}
+        root_rows = {}
+        turned = {}
 
-        def transpose_x(i):
-            x1_view = x_sb[i][:, U0:X_COLS].rearrange("p (k u c) -> p k c u", k=K1, u=P, c=COMP)
-            x1_ps[i] = bank(1, [P, K1 * COMP, P], BF16, "x1_ps")
+        def transpose_x1(i, c, x1_ps, place):
+            view = x_sb[i][:, U0:X_COLS].rearrange("p (k u c) -> p k c u", k=K1, u=P, c=COMP)
             for k in range(K1):
-                for c in range(COMP):
-                    nc.tensor.transpose(x1_ps[i][:, k * COMP + c, :], x1_view[:, k, c, :], ident_bf16[:])
-            words = x_sb[i][:].bitcast(F32)
-            x0_ps[i] = bank(0, [P, 2, P], F32, "x0_ps")
-            for u in range(2):
-                nc.tensor.transpose(x0_ps[i][:, u, :], words[:, u * P : (u + 1) * P], ident_f32[:])
+                nc.tensor.transpose(x1_ps[:, place * K1 + k, :], view[:, k, c, :], ident_bf16[:])
 
-        def copy_x(i):
-            x1t[i] = three.tile([P, K1 * COMP, P], BF16, name="x1t")
-            nc.scalar.copy(out=x1t[i][:], in_=x1_ps[i][:])
+        def turn_x0(first):
+            x0_ps[first] = bank(0, [P, 2, 2, P], F32, "x0_ps")
+            for i in range(2):
+                words = x_sb[first + i][:].bitcast(F32)
+                for u in range(2):
+                    nc.tensor.transpose(x0_ps[first][:, i, u, :], words[:, u * P : (u + 1) * P], ident_f32[:])
+
+        def copy_x0(first):
             nc.vector.tensor_copy(
-                out=x0_grp[:, i, :].bitcast(F32).rearrange("p (n u) -> p n u", u=2),
-                in_=x0_ps[i][:].rearrange("p u n -> p n u"),
+                out=x0_grp[:, first : first + 2, :].bitcast(F32).rearrange("p i (n u) -> p i n u", u=2),
+                in_=x0_ps[first][:].rearrange("p i u n -> p i n u"),
             )
 
-        def multiply_y1(i):
+        def turn_x1(i):
+            x1_ps[i] = bank(1, [P, COMP * K1, P], BF16, "x1_ps")
             for c in range(COMP):
-                y1_bank[i, c] = bank(2 + COMP * (i % 2) + c, [P, PACK, P], F32, "y1_ps")
+                transpose_x1(i, c, x1_ps[i], c)
+
+        def copy_x1(i):
+            x1t[i] = keep.tile([P, COMP * K1, P], BF16, name="x1t%d" % i)
+            if i in VECTOR_COPIES:
+                nc.vector.tensor_copy(out=x1t[i][:], in_=x1_ps[i][:])
+            else:
+                nc.scalar.copy(out=x1t[i][:], in_=x1_ps[i][:])
+
+        def bring_first_x1():
+            first_ps = [bank(1, [P, K1, P], BF16, "first_ps"), bank(0, [P, 2 * K1, P], BF16, "second_ps")]
+            x1t[0] = keep.tile([P, COMP * K1, P], BF16, name="x1t0")
+            transpose_x1(0, 0, first_ps[0], 0)
+            nc.scalar.copy(out=x1t[0][:, 0:K1, :], in_=first_ps[0][:])
+            for c in range(1, COMP):
+                transpose_x1(0, c, first_ps[1], c - 1)
+            nc.vector.tensor_copy(out=x1t[0][:, K1:, :], in_=first_ps[1][:])
+
+        def multiply_y1(i, first=0, end=COMP, again=False):
+            for c in range(first, end):
+                y1_bank[i, c] = bank(5 if again else 2 + COMP * (i % 2) + c, [P, PACK, P], F32, "y1_ps")
                 for t in range(PACK):
                     for k in range(K1):
                         nc.tensor.matmul(
                             y1_bank[i, c][:, t, :],
                             lhsT=w1l1_sb[:, k, t * P : (t + 1) * P],
-                            rhs=x1t[i][:, k * COMP + c, :],
+                            rhs=x1t[i][:, c * K1 + k, :],
                             start=(k == 0),
                             stop=(k == K1 - 1),
                         )
 
-        def park_y1(i):
-            for c in range(COMP):
-                to_sbuf = y1_sb[:, i, c, :].rearrange("p (n t) -> p n t", t=PACK)
-                from_psum = y1_bank[i, c][:].rearrange("p t n -> p n t")
-                if c == 0:
-                    nc.scalar.activation(out=to_sbuf, in_=from_psum, func=FUNC.Copy, scale=S_Y1)
-                else:
-                    nc.vector.tensor_scalar(out=to_sbuf, in0=from_psum, scalar1=S_Y1, scalar2=None, op0=ALU.mult)
+        def park_y1(i, c, on_scalar):
+            to_sbuf = y1_sb[:, PARKED.index(i), c, :].rearrange("p (n t) -> p n t", t=PACK)
+            from_psum = y1_bank[i, c][:].rearrange("p t n -> p n t")
+            if on_scalar:
+                nc.scalar.activation(out=to_sbuf, in_=from_psum, func=FUNC.Copy, scale=S_Y1)
+            else:
+                nc.vector.tensor_scalar(out=to_sbuf, in0=from_psum, scalar1=S_Y1, scalar2=None, op0=ALU.mult)
 
         def square_y1(i):
             squares[i] = three.tile([P, COMP, F1], F32, name="squares")
-            nc.scalar.activation(out=squares[i][:], in_=y1_sb[:, i, :, :], func=FUNC.Square)
+            for c in range(COMP):
+                from_psum = y1_bank[i, c][:]
+                nc.scalar.activation(
+                    out=squares[i][:, c, :].rearrange("p (t n) -> p t n", t=PACK)
+                    if i in TENSOR_SUMS
+                    else squares[i][:, c, :].rearrange("p (n t) -> p n t", t=PACK),
+                    in_=from_psum if i in TENSOR_SUMS else from_psum.rearrange("p t n -> p n t"),
+                    func=FUNC.Square,
+                    scale=S_Y1,
+                )
 
         def add_squares_first(i):
             nc.vector.tensor_tensor(
@@ -153,8 +224,30 @@ def tile_intermodule_pa_kernel(tc, x, w1_l0, w1_l1, w2_l0, w2_l1, out):
         def add_squares_last(i):
             nc.vector.tensor_tensor(out=gate1[:, i, :], in0=gate1[:, i, :], in1=squares[i][:, 2, :], op=ALU.add)
 
+        def sum_on_tensor(i):
+            sums[i] = bank(i % 2, [P, PACK, P], F32, "sums_ps")
+            for t in range(PACK):
+                for c in range(COMP):
+                    nc.tensor.matmul(
+                        sums[i][:, t, :],
+                        lhsT=squares[i][:, c, t * P : (t + 1) * P],
+                        rhs=ident_f32[:],
+                        start=(c == 0),
+                        stop=(c == COMP - 1),
+                        is_transpose=True,
+                    )
+
         def root(i):
-            nc.scalar.activation(out=gate1[:, i, :], in_=gate1[:, i, :], func=FUNC.Sqrt, bias=tiny[:])
+            if i in TENSOR_SUMS:
+                root_rows[i] = keep.tile([P, PACK, P], F32, name="root_rows%d" % i)
+                nc.scalar.activation(out=root_rows[i][:], in_=sums[i][:], func=FUNC.Sqrt, bias=tiny[:])
+            else:
+                nc.scalar.activation(out=gate1[:, i, :], in_=gate1[:, i, :], func=FUNC.Sqrt, bias=tiny[:])
+
+        def turn_root(i):
+            turned[i] = bank(i % 2 if i in KEPT else 5, [P, PACK, P], F32, "turned_ps")
+            for t in range(PACK):
+                nc.tensor.transpose(turned[i][:, t, :], root_rows[i][:, t, :], ident_f32[:])
 
         def quantise_x0(first, count):
             quantise(
@@ -174,10 +267,14 @@ def tile_intermodule_pa_kernel(tc, x, w1_l0, w1_l1, w2_l0, w2_l1, out):
         o0_bank = {}
         o1_bank = {}
         staged = {}
+        order = KEPT + AGAIN + PARKED
+        place = {i: j for j, i in enumerate(order)}
+        Y0_BANKS = ((0, 1), (2, 3))
+        O1_BANKS = (6, 7)
 
-        def multiply_y0(i):
-            for g in range(PASSES0):
-                y0_bank[i, g] = bank(PASSES0 * (i % 2) + g, [P, PACK, P], F32, "y0_ps")
+        def multiply_y0(i, first=0, end=PASSES0):
+            for g in range(first, end):
+                y0_bank[i, g] = bank(Y0_BANKS[place[i] % 2][g], [P, PACK, P], F32, "y0_ps")
                 for t in range(PACK):
                     cols = slice((g * PACK + t) * P, (g * PACK + t + 1) * P)
                     nc.tensor.matmul_mx(
@@ -200,20 +297,41 @@ def tile_intermodule_pa_kernel(tc, x, w1_l0, w1_l1, w2_l0, w2_l1, out):
                     scale=S_Y0,
                 )
 
-        def sigmoids(i):
-            nc.scalar.activation(out=gate1[:, i, :], in_=gate1[:, i, :], func=FUNC.Sigmoid)
+        def sigmoid_y1(i):
+            if i not in TENSOR_SUMS:
+                nc.scalar.activation(out=gate1[:, i, :], in_=gate1[:, i, :], func=FUNC.Sigmoid)
+            else:
+                nc.scalar.activation(
+                    out=gate1[:, i, :].rearrange("p (n t) -> p n t", t=PACK),
+                    in_=turned[i][:].rearrange("p t n -> p n t"),
+                    func=FUNC.Sigmoid,
+                )
+
+        def sigmoid_y0(i):
             nc.scalar.activation(out=gate0[i][:], in_=gate0[i][:], func=FUNC.Sigmoid)
 
-        def gate_y1(i):
-            h1_grp[i] = two.tile([P, COMP, F1], BF16, name="h1_grp", align_bytes=64)
-            nc.vector.tensor_tensor(
-                out=h1_grp[i][:],
-                in0=y1_sb[:, i, :, :],
-                in1=gate1[:, i, :].unsqueeze(1).to_broadcast([P, COMP, F1]),
-                op=ALU.mult,
-            )
-            h1_codes[i] = two.tile([P, COMP, P], U32, name="h1_codes", align_bytes=64)
-            h1_scales[i] = two.tile([P, COMP, P], U8, name="h1_scales", align_bytes=64)
+        def gate_y1(i, first=0, end=COMP):
+            if first == 0:
+                h1_grp[i] = two.tile([P, COMP, F1], BF16, name="h1_grp", align_bytes=64)
+                h1_codes[i] = two.tile([P, COMP, P], U32, name="h1_codes", align_bytes=64)
+                h1_scales[i] = two.tile([P, COMP, P], U8, name="h1_scales", align_bytes=64)
+            if i in PARKED:
+                nc.vector.tensor_tensor(
+                    out=h1_grp[i][:, first:end, :],
+                    in0=y1_sb[:, PARKED.index(i), first:end, :],
+                    in1=gate1[:, i, :].unsqueeze(1).to_broadcast([P, end - first, F1]),
+                    op=ALU.mult,
+                )
+            else:
+                for c in range(first, end):
+                    nc.vector.scalar_tensor_tensor(
+                        out=h1_grp[i][:, c, :].rearrange("p (n t) -> p n t", t=PACK),
+                        in0=y1_bank[i, c][:].rearrange("p t n -> p n t"),
+                        scalar=S_Y1,
+                        in1=gate1[:, i, :].rearrange("p (n t) -> p n t", t=PACK),
+                        op0=ALU.mult,
+                        op1=ALU.mult,
+                    )
 
         def gate_y0(i, g):
             if g == 0:
@@ -245,7 +363,7 @@ def tile_intermodule_pa_kernel(tc, x, w1_l0, w1_l1, w2_l0, w2_l1, out):
 
         def multiply_o1(i):
             for h in range(HALVES):
-                o1_bank[i, h] = bank(6 + h, [P, COMP, P], F32, "o1_ps")
+                o1_bank[i, h] = bank(O1_BANKS[h], [P, COMP, P], F32, "o1_ps")
                 for c in range(COMP):
                     nc.tensor.matmul_mx(
                         out=o1_bank[i, h][:, c, :],
@@ -258,7 +376,7 @@ def tile_intermodule_pa_kernel(tc, x, w1_l0, w1_l1, w2_l0, w2_l1, out):
                     )
 
         def multiply_o0(i):
-            o0_bank[i] = bank(4 + i % 2, [P, U0], F32, "o0_ps")
+            o0_bank[i] = bank(4, [P, U0], F32, "o0_ps")
             for g in range(PASSES0):
                 nc.tensor.matmul_mx(
                     out=o0_bank[i][:],
@@ -291,76 +409,134 @@ def tile_intermodule_pa_kernel(tc, x, w1_l0, w1_l1, w2_l0, w2_l1, out):
 
         half = F0 // 2
 
-        def regroup_w1(a):
-            regroup(w1_grp[:, a * half : (a + 1) * half, :], w1_raw[:, :, a * half : (a + 1) * half])
+        def regroup_w1(a, on_gpsimd=False):
+            regroup(w1_grp[:, a * half : (a + 1) * half, :], w1_raw[:, :, a * half : (a + 1) * half], on_gpsimd)
+
+        def regroup_on_gpsimd(grouped, raw, width):
+            for first in range(0, width, PIECE):
+                cols = slice(first, first + PIECE)
+                regroup(grouped[:, cols, :], raw[:, :, cols], on_gpsimd=True)
 
         def quantise_w1(a):
             cols = slice(a * half, (a + 1) * half)
             quantise(w1_codes[:, cols], w1_scales[:, cols], w1_grp[:, cols, :].rearrange("p w t -> p (w t)"))
 
-        preparation = [
-            lambda: regroup_w1(0),
-            lambda: regroup_w1(1),
-            lambda: quantise_w1(0),
-            lambda: quantise_w1(1),
-            lambda: quantise_x0(0, TILES // 2),
-            lambda: quantise_x0(TILES // 2, TILES // 2),
-        ]
-
-        regroup(v2_grp[:], v2_raw[:])
-        quantise(v2_codes[:], v2_scales[:], v2_grp[:].rearrange("p w t -> p (w t)"))
-
-        for i in range(2):
-            transpose_x(i)
-            copy_x(i)
-        for i in range(TILES):
-            multiply_y1(i)
-            if i + 2 < TILES:
-                transpose_x(i + 2)
-            park_y1(i)
-            if i + 2 < TILES:
-                copy_x(i + 2)
-            if i >= 1:
-                add_squares_first(i - 1)
-            if i < len(preparation):
-                preparation[i]()
-            if i >= 1:
-                add_squares_last(i - 1)
-            if i >= 2:
-                root(i - 2)
-            square_y1(i)
-
-        add_squares_first(TILES - 1)
-        add_squares_last(TILES - 1)
-        for i in range(2):
-            multiply_y0(i)
-        abs_y0(0)
-        for i in range(TILES - 2, TILES):
-            root(i)
-        for g in range(PASSES0):
+        def regroup_w2(g):
             regroup(w2_grp[:, g, :, :], w2_raw[:, g * PACK : (g + 1) * PACK, :])
-        for g in range(PASSES0):
-            quantise(w2_codes[:, g, :], w2_scales[:, g, :], w2_grp[:, g, :, :].rearrange("p w t -> p (w t)"))
-        sigmoids(0)
-        abs_y0(1)
 
+        def quantise_w2(g):
+            quantise(w2_codes[:, g, :], w2_scales[:, g, :], w2_grp[:, g, :, :].rearrange("p w t -> p (w t)"))
+
+        preparation = {
+            5: lambda: quantise_x0(0, TILES // 2),
+            6: lambda: (quantise_x0(TILES // 2, TILES // 2), quantise_w1(0)),
+            7: lambda: quantise_w1(1),
+        }
+
+        regroup_on_gpsimd(w1_grp, w1_raw, F0)
+        for g in range(PASSES0):
+            regroup_on_gpsimd(w2_grp[:, g, :, :], w2_raw[:, g * PACK : (g + 1) * PACK, :], U0)
+        bring_first_x1()
+        multiply_y1(0)
+        turn_x1(1)
+        regroup(v2_grp[:], v2_raw[:])
         for i in range(TILES):
-            if i + 1 < TILES:
-                sigmoids(i + 1)
-            if i > 0:
-                finish_on_scalar(i - 1)
-            gate_y1(i)
-            if i > 0:
-                finish_on_vector(i - 1)
-            gate_y0(i, 0)
-            quantise_h1(i, 0, 2)
-            gate_y0(i, 1)
-            quantise_h1(i, 2, 1)
-            quantise_h0(i)
+            if i == 0:
+                copy_x1(1)
+                quantise(v2_codes[:], v2_scales[:], v2_grp[:].rearrange("p w t -> p (w t)"))
             if i + 2 < TILES:
-                multiply_y0(i + 2)
-                abs_y0(i + 2)
-            multiply_o1(i)
-            multiply_o0(i)
-        finish_on_scalar(TILES - 1)
-        finish_on_vector(TILES - 1)
+                turn_x1(i + 2)
+            if i + 1 < TILES:
+                multiply_y1(i + 1)
+            if i < TILES // 2:
+                turn_x0(2 * i)
+            if i - 1 in TENSOR_SUMS:
+                sum_on_tensor(i - 1)
+            square_y1(i)
+            if i in PARKED:
+                for c in range(COMP):
+                    park_y1(i, c, c == COMP - 1 and i in SCALAR_PARKS)
+            if i + 2 < TILES:
+                copy_x1(i + 2)
+            if i >= 2 and i - 2 not in LATE_ROOTS + TENSOR_SUMS:
+                root(i - 2)
+            if i - 1 in TENSOR_SUMS:
+                root(i - 1)
+            if i not in TENSOR_SUMS:
+                add_squares_first(i)
+            if i < TILES // 2:
+                copy_x0(2 * i)
+            if i in preparation:
+                preparation[i]()
+            if i not in TENSOR_SUMS:
+                add_squares_last(i)
+        sum_on_tensor(TILES - 1)
+        for i in LATE_ROOTS:
+            root(i)
+        turn_root(order[0])
+        root(TILES - 1)
+        turn_root(order[1])
+        for g in range(PASSES0):
+            quantise_w2(g)
+        sigmoid_y1(order[0])
+        sigmoid_y1(order[1])
+        multiply_y0(order[0])
+        abs_y0(order[0])
+        sigmoid_y0(order[0])
+        for i in KEPT:
+            gate_y1(i)
+            if i == order[0]:
+                multiply_y0(order[1])
+                abs_y0(order[1])
+
+        for j, i in enumerate(order):
+            following = order[j + 1] if j + 1 < TILES else None
+            second = order[j + 2] if j + 2 < TILES else None
+            if j + 1 < TILES:
+                if j >= 1:
+                    sigmoid_y1(following)
+                sigmoid_y0(following)
+            if j > 0:
+                finish_on_scalar(order[j - 1])
+            if i in AGAIN:
+                gate_y1(i, 0, 1)
+                multiply_y1(i, 1, 2, again=True)
+                gate_y0(i, 0)
+                if second is not None:
+                    multiply_y0(second, 0, 1)
+                finish_on_vector(order[j - 1])
+                gate_y1(i, 1, 2)
+                multiply_y1(i, 2, 3, again=True)
+                gate_y0(i, 1)
+                if second is not None:
+                    multiply_y0(second, 1, 2)
+                quantise_h1(i, 0, 2)
+                quantise_h0(i)
+                gate_y1(i, 2, 3)
+                if following in AGAIN:
+                    multiply_y1(following, 0, 1, again=True)
+                multiply_o0(i)
+                quantise_h1(i, 2, 1)
+                multiply_o1(i)
+            else:
+                if i in PARKED:
+                    gate_y1(i)
+                if following in AGAIN:
+                    multiply_y1(following, 0, 1, again=True)
+                gate_y0(i, 0)
+                if second is not None:
+                    multiply_y0(second, 0, 1)
+                quantise_h1(i, 0, 2)
+                gate_y0(i, 1)
+                if second is not None:
+                    multiply_y0(second, 1, 2)
+                if j > 0:
+                    finish_on_vector(order[j - 1])
+                quantise_h1(i, 2, 1)
+                multiply_o1(i)
+                quantise_h0(i)
+                multiply_o0(i)
+            if second is not None:
+                abs_y0(second)
+        finish_on_scalar(order[-1])
+        finish_on_vector(order[-1])

@@ -30,10 +30,9 @@ PARKED = [0, 1, 2, 3]
 AGAIN = [4, 5]
 KEPT = [6, 7]
 TENSOR_SUMS = [6, 7]
-PIECE = 64
 VECTOR_COPIES = [1, 2]
 LATE_ROOTS = [4, 5]
-SCALAR_PARKS = [0, 1, 2, 3]
+SCALAR_PARKS = [2, 3]
 WARM_UP = 18
 TINY = 1e-30
 
@@ -103,16 +102,11 @@ def tile_intermodule_pa_kernel(tc, x, w1_l0, w1_l1, w2_l0, w2_l1, out):
         y1_sb = keep.tile([P, len(PARKED), COMP, F1], F32, name="y1_sb")
         gate1 = keep.tile([P, TILES, F1], F32, name="gate1")
 
-        def regroup(grouped, raw, on_gpsimd=False):
-            if on_gpsimd:
-                nc.gpsimd.tensor_scalar(
-                    out=grouped, in0=raw.rearrange("p t w -> p w t"), scalar1=1.0, scalar2=0.0, op0=ALU.mult, op1=ALU.add
-                )
-            else:
-                nc.vector.tensor_copy(
-                    out=grouped.rearrange("p (c i) t -> p c t i", i=4),
-                    in_=raw.rearrange("p t (c i) -> p c t i", i=4),
-                )
+        def regroup(grouped, raw):
+            nc.vector.tensor_copy(
+                out=grouped.rearrange("p (c i) t -> p c t i", i=4),
+                in_=raw.rearrange("p t (c i) -> p c t i", i=4),
+            )
 
         def quantise(codes, scales, grouped):
             nc.vector.quantize_mx(out=codes.bitcast(FP8X4), scales=scales, in_=grouped)
@@ -409,13 +403,8 @@ def tile_intermodule_pa_kernel(tc, x, w1_l0, w1_l1, w2_l0, w2_l1, out):
 
         half = F0 // 2
 
-        def regroup_w1(a, on_gpsimd=False):
-            regroup(w1_grp[:, a * half : (a + 1) * half, :], w1_raw[:, :, a * half : (a + 1) * half], on_gpsimd)
-
-        def regroup_on_gpsimd(grouped, raw, width):
-            for first in range(0, width, PIECE):
-                cols = slice(first, first + PIECE)
-                regroup(grouped[:, cols, :], raw[:, :, cols], on_gpsimd=True)
+        def regroup_w1(a):
+            regroup(w1_grp[:, a * half : (a + 1) * half, :], w1_raw[:, :, a * half : (a + 1) * half])
 
         def quantise_w1(a):
             cols = slice(a * half, (a + 1) * half)
@@ -428,14 +417,12 @@ def tile_intermodule_pa_kernel(tc, x, w1_l0, w1_l1, w2_l0, w2_l1, out):
             quantise(w2_codes[:, g, :], w2_scales[:, g, :], w2_grp[:, g, :, :].rearrange("p w t -> p (w t)"))
 
         preparation = {
-            5: lambda: quantise_x0(0, TILES // 2),
-            6: lambda: (quantise_x0(TILES // 2, TILES // 2), quantise_w1(0)),
-            7: lambda: quantise_w1(1),
+            4: lambda: regroup_w1(0),
+            5: lambda: regroup_w1(1),
+            6: lambda: (quantise_x0(0, TILES // 2), quantise_w1(0)),
+            7: lambda: (quantise_x0(TILES // 2, TILES // 2), quantise_w1(1)),
         }
 
-        regroup_on_gpsimd(w1_grp, w1_raw, F0)
-        for g in range(PASSES0):
-            regroup_on_gpsimd(w2_grp[:, g, :, :], w2_raw[:, g * PACK : (g + 1) * PACK, :], U0)
         bring_first_x1()
         multiply_y1(0)
         turn_x1(1)
@@ -476,6 +463,8 @@ def tile_intermodule_pa_kernel(tc, x, w1_l0, w1_l1, w2_l0, w2_l1, out):
         turn_root(order[0])
         root(TILES - 1)
         turn_root(order[1])
+        for g in range(PASSES0):
+            regroup_w2(g)
         for g in range(PASSES0):
             quantise_w2(g)
         sigmoid_y1(order[0])

@@ -26,13 +26,12 @@ S_Y0 = 1.0 / math.sqrt(U0)
 S_O0 = 1.0 / math.sqrt(F0)
 S_Y1 = 1.0 / math.sqrt(U1)
 S_O1 = 1.0 / math.sqrt(F1)
-PARKED = [0, 1, 2, 3]
-AGAIN = [4, 5]
 KEPT = [6, 7]
+PARKED = 2
 TENSOR_SUMS = [6, 7]
-VECTOR_COPIES = [1, 2]
 LATE_ROOTS = [4, 5]
-SCALAR_PARKS = [2, 3]
+VECTOR_COPIES = [1, 2]
+SCALAR_PARKS = [4, 5]
 WARM_UP = 18
 TINY = 1e-30
 
@@ -99,8 +98,8 @@ def tile_intermodule_pa_kernel(tc, x, w1_l0, w1_l1, w2_l0, w2_l1, out):
         x0_grp = keep.tile([P, TILES, P * PACK], BF16, name="x0_grp", align_bytes=64)
         x0_codes = keep.tile([P, TILES, P], U32, name="x0_codes", align_bytes=64)
         x0_scales = keep.tile([P, TILES, P], U8, name="x0_scales", align_bytes=64)
-        y1_sb = keep.tile([P, len(PARKED), COMP, F1], F32, name="y1_sb")
-        gate1 = keep.tile([P, TILES, F1], F32, name="gate1")
+        y1_sb = keep.tile([P, TILES - len(KEPT), PARKED, F1], F32, name="y1_sb")
+        gates = keep.tile([P, TILES, PASSES0 + 1, F1], F32, name="gates")
 
         def regroup(grouped, raw):
             nc.vector.tensor_copy(
@@ -190,7 +189,7 @@ def tile_intermodule_pa_kernel(tc, x, w1_l0, w1_l1, w2_l0, w2_l1, out):
                         )
 
         def park_y1(i, c, on_scalar):
-            to_sbuf = y1_sb[:, PARKED.index(i), c, :].rearrange("p (n t) -> p n t", t=PACK)
+            to_sbuf = y1_sb[:, i, c, :].rearrange("p (n t) -> p n t", t=PACK)
             from_psum = y1_bank[i, c][:].rearrange("p t n -> p n t")
             if on_scalar:
                 nc.scalar.activation(out=to_sbuf, in_=from_psum, func=FUNC.Copy, scale=S_Y1)
@@ -212,14 +211,14 @@ def tile_intermodule_pa_kernel(tc, x, w1_l0, w1_l1, w2_l0, w2_l1, out):
 
         def add_squares_first(i):
             nc.vector.tensor_tensor(
-                out=gate1[:, i, :], in0=squares[i][:, 0, :], in1=squares[i][:, 1, :], op=ALU.add
+                out=gates[:, i, PASSES0, :], in0=squares[i][:, 0, :], in1=squares[i][:, 1, :], op=ALU.add
             )
 
         def add_squares_last(i):
-            nc.vector.tensor_tensor(out=gate1[:, i, :], in0=gate1[:, i, :], in1=squares[i][:, 2, :], op=ALU.add)
+            nc.vector.tensor_tensor(out=gates[:, i, PASSES0, :], in0=gates[:, i, PASSES0, :], in1=squares[i][:, 2, :], op=ALU.add)
 
         def sum_on_tensor(i):
-            sums[i] = bank(i % 2, [P, PACK, P], F32, "sums_ps")
+            sums[i] = bank(i % 2 if i in KEPT else 0, [P, PACK, P], F32, "sums_ps")
             for t in range(PACK):
                 for c in range(COMP):
                     nc.tensor.matmul(
@@ -236,7 +235,7 @@ def tile_intermodule_pa_kernel(tc, x, w1_l0, w1_l1, w2_l0, w2_l1, out):
                 root_rows[i] = keep.tile([P, PACK, P], F32, name="root_rows%d" % i)
                 nc.scalar.activation(out=root_rows[i][:], in_=sums[i][:], func=FUNC.Sqrt, bias=tiny[:])
             else:
-                nc.scalar.activation(out=gate1[:, i, :], in_=gate1[:, i, :], func=FUNC.Sqrt, bias=tiny[:])
+                nc.scalar.activation(out=gates[:, i, PASSES0, :], in_=gates[:, i, PASSES0, :], func=FUNC.Sqrt, bias=tiny[:])
 
         def turn_root(i):
             turned[i] = bank(i % 2 if i in KEPT else 5, [P, PACK, P], F32, "turned_ps")
@@ -251,17 +250,15 @@ def tile_intermodule_pa_kernel(tc, x, w1_l0, w1_l1, w2_l0, w2_l1, out):
             )
 
         y0_bank = {}
-        gate0 = {}
-        h0_codes = {}
-        h0_scales = {}
-        h1_codes = {}
-        h1_scales = {}
-        h0_grp = {}
-        h1_grp = {}
+        h_grp = {}
+        h_codes = {}
+        h_scales = {}
+        H1_PLACE = (0, 1, 4)
+        H0_PLACE = 2
         o0_bank = {}
         o1_bank = {}
         staged = {}
-        order = KEPT + AGAIN + PARKED
+        order = KEPT + list(range(TILES - len(KEPT)))
         place = {i: j for j, i in enumerate(order)}
         Y0_BANKS = ((0, 1), (2, 3))
         O1_BANKS = (6, 7)
@@ -282,77 +279,62 @@ def tile_intermodule_pa_kernel(tc, x, w1_l0, w1_l1, w2_l0, w2_l1, out):
                     )
 
         def abs_y0(i):
-            gate0[i] = two.tile([P, PASSES0, F1], F32, name="gate0")
             for g in range(PASSES0):
                 nc.scalar.activation(
-                    out=gate0[i][:, g, :].rearrange("p (n t) -> p n t", t=PACK),
+                    out=gates[:, i, g, :].rearrange("p (n t) -> p n t", t=PACK),
                     in_=y0_bank[i, g][:].rearrange("p t n -> p n t"),
                     func=FUNC.Abs,
                     scale=S_Y0,
                 )
 
-        def sigmoid_y1(i):
-            if i not in TENSOR_SUMS:
-                nc.scalar.activation(out=gate1[:, i, :], in_=gate1[:, i, :], func=FUNC.Sigmoid)
-            else:
-                nc.scalar.activation(
-                    out=gate1[:, i, :].rearrange("p (n t) -> p n t", t=PACK),
-                    in_=turned[i][:].rearrange("p t n -> p n t"),
-                    func=FUNC.Sigmoid,
-                )
+        def sigmoids(i, first=0, end=PASSES0 + 1):
+            nc.scalar.activation(out=gates[:, i, first:end, :], in_=gates[:, i, first:end, :], func=FUNC.Sigmoid)
 
-        def sigmoid_y0(i):
-            nc.scalar.activation(out=gate0[i][:], in_=gate0[i][:], func=FUNC.Sigmoid)
+        def sigmoid_turned(i):
+            nc.scalar.activation(
+                out=gates[:, i, PASSES0, :].rearrange("p (n t) -> p n t", t=PACK),
+                in_=turned[i][:].rearrange("p t n -> p n t"),
+                func=FUNC.Sigmoid,
+            )
 
-        def gate_y1(i, first=0, end=COMP):
-            if first == 0:
-                h1_grp[i] = two.tile([P, COMP, F1], BF16, name="h1_grp", align_bytes=64)
-                h1_codes[i] = two.tile([P, COMP, P], U32, name="h1_codes", align_bytes=64)
-                h1_scales[i] = two.tile([P, COMP, P], U8, name="h1_scales", align_bytes=64)
-            if i in PARKED:
-                nc.vector.tensor_tensor(
-                    out=h1_grp[i][:, first:end, :],
-                    in0=y1_sb[:, PARKED.index(i), first:end, :],
-                    in1=gate1[:, i, :].unsqueeze(1).to_broadcast([P, end - first, F1]),
-                    op=ALU.mult,
-                )
-            else:
-                for c in range(first, end):
-                    nc.vector.scalar_tensor_tensor(
-                        out=h1_grp[i][:, c, :].rearrange("p (n t) -> p n t", t=PACK),
-                        in0=y1_bank[i, c][:].rearrange("p t n -> p n t"),
-                        scalar=S_Y1,
-                        in1=gate1[:, i, :].rearrange("p (n t) -> p n t", t=PACK),
-                        op0=ALU.mult,
-                        op1=ALU.mult,
-                    )
+        def open_tile(i):
+            h_grp[i] = two.tile([P, 5, F1], BF16, name="h_grp", align_bytes=64)
+            h_codes[i] = two.tile([P, 5, P], U32, name="h_codes", align_bytes=64)
+            h_scales[i] = two.tile([P, 5, P], U8, name="h_scales", align_bytes=64)
 
-        def gate_y0(i, g):
-            if g == 0:
-                h0_grp[i] = two.tile([P, PASSES0, F1], BF16, name="h0_grp", align_bytes=64)
+        def gate_parked(i):
+            nc.vector.tensor_tensor(
+                out=h_grp[i][:, 0:PARKED, :],
+                in0=y1_sb[:, i, :, :],
+                in1=gates[:, i, PASSES0, :].unsqueeze(1).to_broadcast([P, PARKED, F1]),
+                op=ALU.mult,
+            )
+
+        def gate_in_psum(i, c):
             nc.vector.scalar_tensor_tensor(
-                out=h0_grp[i][:, g, :].rearrange("p (n t) -> p n t", t=PACK),
-                in0=y0_bank[i, g][:].rearrange("p t n -> p n t"),
-                scalar=S_Y0,
-                in1=gate0[i][:, g, :].rearrange("p (n t) -> p n t", t=PACK),
+                out=h_grp[i][:, H1_PLACE[c], :].rearrange("p (n t) -> p n t", t=PACK),
+                in0=y1_bank[i, c][:].rearrange("p t n -> p n t"),
+                scalar=S_Y1,
+                in1=gates[:, i, PASSES0, :].rearrange("p (n t) -> p n t", t=PACK),
                 op0=ALU.mult,
                 op1=ALU.mult,
             )
 
-        def quantise_h1(i, first, count):
-            quantise(
-                h1_codes[i][:, first : first + count, :].rearrange("p c n -> p (c n)"),
-                h1_scales[i][:, first : first + count, :].rearrange("p c n -> p (c n)"),
-                h1_grp[i][:, first : first + count, :].rearrange("p c f -> p (c f)"),
+        def gate_y0(i, g):
+            nc.vector.scalar_tensor_tensor(
+                out=h_grp[i][:, H0_PLACE + g, :].rearrange("p (n t) -> p n t", t=PACK),
+                in0=y0_bank[i, g][:].rearrange("p t n -> p n t"),
+                scalar=S_Y0,
+                in1=gates[:, i, g, :].rearrange("p (n t) -> p n t", t=PACK),
+                op0=ALU.mult,
+                op1=ALU.mult,
             )
 
-        def quantise_h0(i):
-            h0_codes[i] = two.tile([P, PASSES0, P], U32, name="h0_codes", align_bytes=64)
-            h0_scales[i] = two.tile([P, PASSES0, P], U8, name="h0_scales", align_bytes=64)
+        def quantise_h(i, first, count):
             quantise(
-                h0_codes[i][:].rearrange("p g n -> p (g n)"),
-                h0_scales[i][:].rearrange("p g n -> p (g n)"),
-                h0_grp[i][:].rearrange("p g f -> p (g f)"),
+                h_codes[i][:, first : first + count, :].rearrange("p c n -> p (c n)"),
+                h_scales[i][:, first : first + count, :].rearrange("p c n -> p (c n)"),
+                h_grp[i][:, first : first + count, :].rearrange("p c f -> p (c f)"),
             )
 
         def multiply_o1(i):
@@ -361,8 +343,8 @@ def tile_intermodule_pa_kernel(tc, x, w1_l0, w1_l1, w2_l0, w2_l1, out):
                 for c in range(COMP):
                     nc.tensor.matmul_mx(
                         out=o1_bank[i, h][:, c, :],
-                        lhsT=h1_codes[i][:, c, :].bitcast(FP8X4),
-                        lhsT_scale=h1_scales[i][:, c, :],
+                        lhsT=h_codes[i][:, H1_PLACE[c], :].bitcast(FP8X4),
+                        lhsT_scale=h_scales[i][:, H1_PLACE[c], :],
                         rhs=v2_codes[:, h * P : (h + 1) * P].bitcast(FP8X4),
                         rhs_scale=v2_scales[:, h * P : (h + 1) * P],
                         start=True,
@@ -374,8 +356,8 @@ def tile_intermodule_pa_kernel(tc, x, w1_l0, w1_l1, w2_l0, w2_l1, out):
             for g in range(PASSES0):
                 nc.tensor.matmul_mx(
                     out=o0_bank[i][:],
-                    lhsT=h0_codes[i][:, g, :].bitcast(FP8X4),
-                    lhsT_scale=h0_scales[i][:, g, :],
+                    lhsT=h_codes[i][:, H0_PLACE + g, :].bitcast(FP8X4),
+                    lhsT_scale=h_scales[i][:, H0_PLACE + g, :],
                     rhs=w2_codes[:, g, :].bitcast(FP8X4),
                     rhs_scale=w2_scales[:, g, :],
                     start=(g == 0),
@@ -389,14 +371,16 @@ def tile_intermodule_pa_kernel(tc, x, w1_l0, w1_l1, w2_l0, w2_l1, out):
                 o1_bank[i, h][:].rearrange("p c w -> p w c"),
             )
 
-        def finish_on_scalar(i):
+        def finish_o0(i):
             staged[i] = three.tile([P, X_COLS], F32, name="staged")
-            to_sbuf, from_psum = o1_views(i, 0)
-            nc.scalar.activation(out=to_sbuf, in_=from_psum, func=FUNC.Copy, scale=S_O1)
             nc.scalar.activation(out=staged[i][:, 0:U0], in_=o0_bank[i][:], func=FUNC.Copy, scale=S_O0)
             nc.sync.dma_start(out=out[i * P : (i + 1) * P, 0:U0], in_=staged[i][:, 0:U0])
 
-        def finish_on_vector(i):
+        def finish_o1_on_scalar(i):
+            to_sbuf, from_psum = o1_views(i, 0)
+            nc.scalar.activation(out=to_sbuf, in_=from_psum, func=FUNC.Copy, scale=S_O1)
+
+        def finish_o1_on_vector(i):
             to_sbuf, from_psum = o1_views(i, 1)
             nc.vector.tensor_scalar(out=to_sbuf, in0=from_psum, scalar1=S_O1, scalar2=None, op0=ALU.mult)
             nc.sync.dma_start(out=out[i * P : (i + 1) * P, U0:X_COLS], in_=staged[i][:, U0:X_COLS])
@@ -440,9 +424,9 @@ def tile_intermodule_pa_kernel(tc, x, w1_l0, w1_l1, w2_l0, w2_l1, out):
             if i - 1 in TENSOR_SUMS:
                 sum_on_tensor(i - 1)
             square_y1(i)
-            if i in PARKED:
-                for c in range(COMP):
-                    park_y1(i, c, c == COMP - 1 and i in SCALAR_PARKS)
+            if i not in KEPT:
+                for c in range(PARKED):
+                    park_y1(i, c, c == PARKED - 1 and i in SCALAR_PARKS)
             if i + 2 < TILES:
                 copy_x1(i + 2)
             if i >= 2 and i - 2 not in LATE_ROOTS + TENSOR_SUMS:
@@ -467,65 +451,57 @@ def tile_intermodule_pa_kernel(tc, x, w1_l0, w1_l1, w2_l0, w2_l1, out):
             regroup_w2(g)
         for g in range(PASSES0):
             quantise_w2(g)
-        sigmoid_y1(order[0])
-        sigmoid_y1(order[1])
+        sigmoid_turned(order[0])
+        sigmoid_turned(order[1])
         multiply_y0(order[0])
         abs_y0(order[0])
-        sigmoid_y0(order[0])
+        sigmoids(order[0], 0, PASSES0)
         for i in KEPT:
-            gate_y1(i)
+            open_tile(i)
+            for c in range(COMP):
+                gate_in_psum(i, c)
             if i == order[0]:
                 multiply_y0(order[1])
                 abs_y0(order[1])
 
         for j, i in enumerate(order):
+            before = order[j - 1] if j > 0 else None
             following = order[j + 1] if j + 1 < TILES else None
             second = order[j + 2] if j + 2 < TILES else None
-            if j + 1 < TILES:
-                if j >= 1:
-                    sigmoid_y1(following)
-                sigmoid_y0(following)
-            if j > 0:
-                finish_on_scalar(order[j - 1])
-            if i in AGAIN:
-                gate_y1(i, 0, 1)
-                multiply_y1(i, 1, 2, again=True)
-                gate_y0(i, 0)
-                if second is not None:
-                    multiply_y0(second, 0, 1)
-                finish_on_vector(order[j - 1])
-                gate_y1(i, 1, 2)
-                multiply_y1(i, 2, 3, again=True)
-                gate_y0(i, 1)
-                if second is not None:
-                    multiply_y0(second, 1, 2)
-                quantise_h1(i, 0, 2)
-                quantise_h0(i)
-                gate_y1(i, 2, 3)
-                if following in AGAIN:
-                    multiply_y1(following, 0, 1, again=True)
+            again = following is not None and following not in KEPT
+            if following is not None:
+                sigmoids(following, 0, PASSES0 + 1 if again else PASSES0)
+            if before is not None:
+                finish_o0(before)
+                finish_o1_on_scalar(before)
+            if i not in KEPT:
+                open_tile(i)
+                if following is not None:
+                    gate_parked(i)
+                    gate_in_psum(i, COMP - 1)
+            if again:
+                multiply_y1(following, PARKED, COMP, again=True)
+            gate_y0(i, 0)
+            if second is not None:
+                multiply_y0(second, 0, 1)
+            gate_y0(i, 1)
+            if second is not None:
+                multiply_y0(second, 1, 2)
+            if before is not None:
+                finish_o1_on_vector(before)
+            if following is None:
+                quantise_h(i, H0_PLACE, PASSES0)
                 multiply_o0(i)
-                quantise_h1(i, 2, 1)
-                multiply_o1(i)
+                finish_o0(i)
+                gate_parked(i)
+                gate_in_psum(i, COMP - 1)
+                quantise_h(i, 0, PARKED)
             else:
-                if i in PARKED:
-                    gate_y1(i)
-                if following in AGAIN:
-                    multiply_y1(following, 0, 1, again=True)
-                gate_y0(i, 0)
-                if second is not None:
-                    multiply_y0(second, 0, 1)
-                quantise_h1(i, 0, 2)
-                gate_y0(i, 1)
-                if second is not None:
-                    multiply_y0(second, 1, 2)
-                if j > 0:
-                    finish_on_vector(order[j - 1])
-                quantise_h1(i, 2, 1)
-                multiply_o1(i)
-                quantise_h0(i)
+                quantise_h(i, 0, 4)
                 multiply_o0(i)
+            quantise_h(i, 4, 1)
+            multiply_o1(i)
             if second is not None:
                 abs_y0(second)
-        finish_on_scalar(order[-1])
-        finish_on_vector(order[-1])
+        finish_o1_on_scalar(order[-1])
+        finish_o1_on_vector(order[-1])

@@ -31,7 +31,8 @@ PARKED = 2
 TENSOR_SUMS = [6, 7]
 LATE_ROOTS = [4, 5]
 VECTOR_COPIES = [1, 2]
-SCALAR_PARKS = [4, 5]
+SCALAR_PARKS = [3, 4, 5]
+VECTOR_FINISHES = [0, 2, 4]
 WARM_UP = 18
 TINY = 1e-30
 
@@ -65,14 +66,16 @@ def tile_intermodule_pa_kernel(tc, x, w1_l0, w1_l1, w2_l0, w2_l1, out):
 
         load_x(0, U0, X_COLS)
         nc.sync.dma_start(out=w1l1_sb[:], in_=w1_l1.rearrange("(k p) v -> p k v", p=P))
+        load_x(1, U0, X_COLS)
         nc.sync.dma_start(out=v2_raw[:], in_=w2_l1.rearrange("(t p) w -> p t w", p=P))
-        load_x(1)
-        load_x(0, 0, U0)
         load_x(2)
-        load_w1(0, F0 // 2)
+        for i in range(2):
+            load_x(i, 0, U0)
         load_x(3)
+        load_w1(0, F0 // 2)
+        load_x(4)
         load_w1(F0 // 2, F0)
-        for i in range(4, TILES):
+        for i in range(5, TILES):
             load_x(i)
         nc.sync.dma_start(out=w2_raw[:], in_=w2_l0.rearrange("(a p) j -> p a j", p=P))
 
@@ -98,7 +101,7 @@ def tile_intermodule_pa_kernel(tc, x, w1_l0, w1_l1, w2_l0, w2_l1, out):
         x0_grp = keep.tile([P, TILES, P * PACK], BF16, name="x0_grp", align_bytes=64)
         x0_codes = keep.tile([P, TILES, P], U32, name="x0_codes", align_bytes=64)
         x0_scales = keep.tile([P, TILES, P], U8, name="x0_scales", align_bytes=64)
-        y1_sb = keep.tile([P, TILES - len(KEPT), PARKED, F1], F32, name="y1_sb")
+        y1_sb = keep.tile([P, TILES - len(KEPT), PARKED, F1], F32, name="y1_sb", align_bytes=64)
         gates = keep.tile([P, TILES, PASSES0 + 1, F1], F32, name="gates")
 
         def regroup(grouped, raw):
@@ -253,7 +256,8 @@ def tile_intermodule_pa_kernel(tc, x, w1_l0, w1_l1, w2_l0, w2_l1, out):
         h_grp = {}
         h_codes = {}
         h_scales = {}
-        H1_PLACE = (0, 1, 4)
+        c1_grp = {}
+        H1_PLACE = (0, 4, 1)
         H0_PLACE = 2
         o0_bank = {}
         o1_bank = {}
@@ -298,21 +302,26 @@ def tile_intermodule_pa_kernel(tc, x, w1_l0, w1_l1, w2_l0, w2_l1, out):
             )
 
         def open_tile(i):
-            h_grp[i] = two.tile([P, 5, F1], BF16, name="h_grp", align_bytes=64)
+            h_grp[i] = two.tile([P, 4, F1], BF16, name="h_grp", align_bytes=64)
             h_codes[i] = two.tile([P, 5, P], U32, name="h_codes", align_bytes=64)
             h_scales[i] = two.tile([P, 5, P], U8, name="h_scales", align_bytes=64)
+            if i in KEPT:
+                c1_kept = two.tile([P, F1], BF16, name="c1_kept", align_bytes=64)
+                c1_grp[i] = c1_kept[:]
+            else:
+                c1_grp[i] = y1_sb[:, i, 0, :].bitcast(BF16)[:, 0:F1]
 
-        def gate_parked(i):
-            nc.vector.tensor_tensor(
-                out=h_grp[i][:, 0:PARKED, :],
-                in0=y1_sb[:, i, :, :],
-                in1=gates[:, i, PASSES0, :].unsqueeze(1).to_broadcast([P, PARKED, F1]),
-                op=ALU.mult,
+        def h1_values(i, c):
+            return c1_grp[i] if c == 1 else h_grp[i][:, H1_PLACE[c], :]
+
+        def gate_parked(i, c, engine):
+            engine.tensor_tensor(
+                out=h1_values(i, c), in0=y1_sb[:, i, c, :], in1=gates[:, i, PASSES0, :], op=ALU.mult
             )
 
         def gate_in_psum(i, c):
             nc.vector.scalar_tensor_tensor(
-                out=h_grp[i][:, H1_PLACE[c], :].rearrange("p (n t) -> p n t", t=PACK),
+                out=h1_values(i, c).rearrange("p (n t) -> p n t", t=PACK),
                 in0=y1_bank[i, c][:].rearrange("p t n -> p n t"),
                 scalar=S_Y1,
                 in1=gates[:, i, PASSES0, :].rearrange("p (n t) -> p n t", t=PACK),
@@ -336,6 +345,9 @@ def tile_intermodule_pa_kernel(tc, x, w1_l0, w1_l1, w2_l0, w2_l1, out):
                 h_scales[i][:, first : first + count, :].rearrange("p c n -> p (c n)"),
                 h_grp[i][:, first : first + count, :].rearrange("p c f -> p (c f)"),
             )
+
+        def quantise_c1(i):
+            quantise(h_codes[i][:, H1_PLACE[1], :], h_scales[i][:, H1_PLACE[1], :], c1_grp[i])
 
         def multiply_o1(i):
             for h in range(HALVES):
@@ -376,13 +388,14 @@ def tile_intermodule_pa_kernel(tc, x, w1_l0, w1_l1, w2_l0, w2_l1, out):
             nc.scalar.activation(out=staged[i][:, 0:U0], in_=o0_bank[i][:], func=FUNC.Copy, scale=S_O0)
             nc.sync.dma_start(out=out[i * P : (i + 1) * P, 0:U0], in_=staged[i][:, 0:U0])
 
-        def finish_o1_on_scalar(i):
-            to_sbuf, from_psum = o1_views(i, 0)
-            nc.scalar.activation(out=to_sbuf, in_=from_psum, func=FUNC.Copy, scale=S_O1)
+        def finish_o1(i, h, engine):
+            to_sbuf, from_psum = o1_views(i, h)
+            if engine is nc.scalar:
+                nc.scalar.activation(out=to_sbuf, in_=from_psum, func=FUNC.Copy, scale=S_O1)
+            else:
+                nc.vector.tensor_scalar(out=to_sbuf, in0=from_psum, scalar1=S_O1, scalar2=None, op0=ALU.mult)
 
-        def finish_o1_on_vector(i):
-            to_sbuf, from_psum = o1_views(i, 1)
-            nc.vector.tensor_scalar(out=to_sbuf, in0=from_psum, scalar1=S_O1, scalar2=None, op0=ALU.mult)
+        def store_o1(i):
             nc.sync.dma_start(out=out[i * P : (i + 1) * P, U0:X_COLS], in_=staged[i][:, U0:X_COLS])
 
         half = F0 // 2
@@ -408,12 +421,13 @@ def tile_intermodule_pa_kernel(tc, x, w1_l0, w1_l1, w2_l0, w2_l1, out):
         }
 
         bring_first_x1()
-        multiply_y1(0)
+        multiply_y1(0, 0, 1)
         turn_x1(1)
+        copy_x1(1)
+        multiply_y1(0, 1, COMP)
         regroup(v2_grp[:], v2_raw[:])
         for i in range(TILES):
-            if i == 0:
-                copy_x1(1)
+            if i == 1:
                 quantise(v2_codes[:], v2_scales[:], v2_grp[:].rearrange("p w t -> p (w t)"))
             if i + 2 < TILES:
                 turn_x1(i + 2)
@@ -469,15 +483,19 @@ def tile_intermodule_pa_kernel(tc, x, w1_l0, w1_l1, w2_l0, w2_l1, out):
             following = order[j + 1] if j + 1 < TILES else None
             second = order[j + 2] if j + 2 < TILES else None
             again = following is not None and following not in KEPT
+            if again:
+                sigmoids(following, PASSES0, PASSES0 + 1)
             if following is not None:
-                sigmoids(following, 0, PASSES0 + 1 if again else PASSES0)
+                sigmoids(following, 0, PASSES0)
             if before is not None:
                 finish_o0(before)
-                finish_o1_on_scalar(before)
+                if before not in VECTOR_FINISHES:
+                    finish_o1(before, 0, nc.scalar)
             if i not in KEPT:
                 open_tile(i)
                 if following is not None:
-                    gate_parked(i)
+                    gate_parked(i, 0, nc.vector)
+                    gate_parked(i, 1, nc.gpsimd)
                     gate_in_psum(i, COMP - 1)
             if again:
                 multiply_y1(following, PARKED, COMP, again=True)
@@ -488,20 +506,25 @@ def tile_intermodule_pa_kernel(tc, x, w1_l0, w1_l1, w2_l0, w2_l1, out):
             if second is not None:
                 multiply_y0(second, 1, 2)
             if before is not None:
-                finish_o1_on_vector(before)
+                if before in VECTOR_FINISHES:
+                    finish_o1(before, 0, nc.vector)
+                finish_o1(before, 1, nc.vector)
+                store_o1(before)
             if following is None:
                 quantise_h(i, H0_PLACE, PASSES0)
                 multiply_o0(i)
                 finish_o0(i)
-                gate_parked(i)
                 gate_in_psum(i, COMP - 1)
-                quantise_h(i, 0, PARKED)
+                gate_parked(i, 0, nc.vector)
+                gate_parked(i, 1, nc.vector)
+                quantise_h(i, 0, H0_PLACE)
             else:
                 quantise_h(i, 0, 4)
                 multiply_o0(i)
-            quantise_h(i, 4, 1)
+            quantise_c1(i)
             multiply_o1(i)
             if second is not None:
                 abs_y0(second)
-        finish_o1_on_scalar(order[-1])
-        finish_o1_on_vector(order[-1])
+        finish_o1(order[-1], 0, nc.scalar)
+        finish_o1(order[-1], 1, nc.vector)
+        store_o1(order[-1])

@@ -31,8 +31,8 @@ PARKED = 2
 TENSOR_SUMS = [6, 7]
 LATE_ROOTS = [4, 5]
 VECTOR_COPIES = [1, 2]
-SCALAR_PARKS = [3, 4, 5]
-VECTOR_FINISHES = [0, 2, 4]
+SCALAR_PARKS = [1, 3, 5]
+VECTOR_FINISHES = [0, 2]
 WARM_UP = 18
 TINY = 1e-30
 
@@ -305,7 +305,7 @@ def tile_intermodule_pa_kernel(tc, x, w1_l0, w1_l1, w2_l0, w2_l1, out):
             h_grp[i] = two.tile([P, 4, F1], BF16, name="h_grp", align_bytes=64)
             h_codes[i] = two.tile([P, 5, P], U32, name="h_codes", align_bytes=64)
             h_scales[i] = two.tile([P, 5, P], U8, name="h_scales", align_bytes=64)
-            if i in KEPT:
+            if i in KEPT or i == order[-1]:
                 c1_kept = two.tile([P, F1], BF16, name="c1_kept", align_bytes=64)
                 c1_grp[i] = c1_kept[:]
             else:
@@ -349,10 +349,11 @@ def tile_intermodule_pa_kernel(tc, x, w1_l0, w1_l1, w2_l0, w2_l1, out):
         def quantise_c1(i):
             quantise(h_codes[i][:, H1_PLACE[1], :], h_scales[i][:, H1_PLACE[1], :], c1_grp[i])
 
-        def multiply_o1(i):
+        def multiply_o1(i, components):
             for h in range(HALVES):
-                o1_bank[i, h] = bank(O1_BANKS[h], [P, COMP, P], F32, "o1_ps")
-                for c in range(COMP):
+                if (i, h) not in o1_bank:
+                    o1_bank[i, h] = bank(O1_BANKS[h], [P, COMP, P], F32, "o1_ps")
+                for c in components:
                     nc.tensor.matmul_mx(
                         out=o1_bank[i, h][:, c, :],
                         lhsT=h_codes[i][:, H1_PLACE[c], :].bitcast(FP8X4),
@@ -491,6 +492,9 @@ def tile_intermodule_pa_kernel(tc, x, w1_l0, w1_l1, w2_l0, w2_l1, out):
                 finish_o0(before)
                 if before not in VECTOR_FINISHES:
                     finish_o1(before, 0, nc.scalar)
+                if following is None:
+                    finish_o1(before, 1, nc.scalar)
+                    store_o1(before)
             if i not in KEPT:
                 open_tile(i)
                 if following is not None:
@@ -505,7 +509,7 @@ def tile_intermodule_pa_kernel(tc, x, w1_l0, w1_l1, w2_l0, w2_l1, out):
             gate_y0(i, 1)
             if second is not None:
                 multiply_y0(second, 1, 2)
-            if before is not None:
+            if before is not None and following is not None:
                 if before in VECTOR_FINISHES:
                     finish_o1(before, 0, nc.vector)
                 finish_o1(before, 1, nc.vector)
@@ -521,8 +525,9 @@ def tile_intermodule_pa_kernel(tc, x, w1_l0, w1_l1, w2_l0, w2_l1, out):
             else:
                 quantise_h(i, 0, 4)
                 multiply_o0(i)
+            multiply_o1(i, (0, 2))
             quantise_c1(i)
-            multiply_o1(i)
+            multiply_o1(i, (1,))
             if second is not None:
                 abs_y0(second)
         finish_o1(order[-1], 0, nc.scalar)

@@ -31,8 +31,9 @@ PARKED = 2
 TENSOR_SUMS = [6, 7]
 LATE_ROOTS = [4, 5]
 VECTOR_COPIES = [1, 2]
-SCALAR_PARKS = [1, 3, 5]
+SCALAR_PARKS = []
 VECTOR_FINISHES = [0, 2]
+GPSIMD_SUMS = [0, 1, 2, 3, 4]
 WARM_UP = 18
 TINY = 1e-30
 
@@ -217,8 +218,8 @@ def tile_intermodule_pa_kernel(tc, x, w1_l0, w1_l1, w2_l0, w2_l1, out):
                 out=gates[:, i, PASSES0, :], in0=squares[i][:, 0, :], in1=squares[i][:, 1, :], op=ALU.add
             )
 
-        def add_squares_last(i):
-            nc.vector.tensor_tensor(out=gates[:, i, PASSES0, :], in0=gates[:, i, PASSES0, :], in1=squares[i][:, 2, :], op=ALU.add)
+        def add_squares_last(i, engine):
+            engine.tensor_tensor(out=gates[:, i, PASSES0, :], in0=gates[:, i, PASSES0, :], in1=squares[i][:, 2, :], op=ALU.add)
 
         def sum_on_tensor(i):
             sums[i] = bank(i % 2 if i in KEPT else 0, [P, PACK, P], F32, "sums_ps")
@@ -305,7 +306,7 @@ def tile_intermodule_pa_kernel(tc, x, w1_l0, w1_l1, w2_l0, w2_l1, out):
             h_grp[i] = two.tile([P, 4, F1], BF16, name="h_grp", align_bytes=64)
             h_codes[i] = two.tile([P, 5, P], U32, name="h_codes", align_bytes=64)
             h_scales[i] = two.tile([P, 5, P], U8, name="h_scales", align_bytes=64)
-            if i in KEPT or i == order[-1]:
+            if i in KEPT:
                 c1_kept = two.tile([P, F1], BF16, name="c1_kept", align_bytes=64)
                 c1_grp[i] = c1_kept[:]
             else:
@@ -396,8 +397,9 @@ def tile_intermodule_pa_kernel(tc, x, w1_l0, w1_l1, w2_l0, w2_l1, out):
             else:
                 nc.vector.tensor_scalar(out=to_sbuf, in0=from_psum, scalar1=S_O1, scalar2=None, op0=ALU.mult)
 
-        def store_o1(i):
-            nc.sync.dma_start(out=out[i * P : (i + 1) * P, U0:X_COLS], in_=staged[i][:, U0:X_COLS])
+        def store_o1(i, first=0, end=HALVES):
+            cols = slice(U0 + first * P * COMP, U0 + end * P * COMP)
+            nc.sync.dma_start(out=out[i * P : (i + 1) * P, cols], in_=staged[i][:, cols])
 
         half = F0 // 2
 
@@ -436,9 +438,12 @@ def tile_intermodule_pa_kernel(tc, x, w1_l0, w1_l1, w2_l0, w2_l1, out):
                 multiply_y1(i + 1)
             if i < TILES // 2:
                 turn_x0(2 * i)
-            if i - 1 in TENSOR_SUMS:
+            if i - 1 in KEPT:
                 sum_on_tensor(i - 1)
             square_y1(i)
+            if i - 1 in GPSIMD_SUMS:
+                add_squares_first(i - 1)
+                add_squares_last(i - 1, nc.gpsimd)
             if i not in KEPT:
                 for c in range(PARKED):
                     park_y1(i, c, c == PARKED - 1 and i in SCALAR_PARKS)
@@ -446,19 +451,18 @@ def tile_intermodule_pa_kernel(tc, x, w1_l0, w1_l1, w2_l0, w2_l1, out):
                 copy_x1(i + 2)
             if i >= 2 and i - 2 not in LATE_ROOTS + TENSOR_SUMS:
                 root(i - 2)
-            if i - 1 in TENSOR_SUMS:
-                root(i - 1)
-            if i not in TENSOR_SUMS:
+            if i not in TENSOR_SUMS + GPSIMD_SUMS:
                 add_squares_first(i)
             if i < TILES // 2:
                 copy_x0(2 * i)
             if i in preparation:
                 preparation[i]()
-            if i not in TENSOR_SUMS:
-                add_squares_last(i)
+            if i not in TENSOR_SUMS + GPSIMD_SUMS:
+                add_squares_last(i, nc.vector)
         sum_on_tensor(TILES - 1)
         for i in LATE_ROOTS:
             root(i)
+        root(TILES - 2)
         turn_root(order[0])
         root(TILES - 1)
         turn_root(order[1])
@@ -497,9 +501,9 @@ def tile_intermodule_pa_kernel(tc, x, w1_l0, w1_l1, w2_l0, w2_l1, out):
                     store_o1(before)
             if i not in KEPT:
                 open_tile(i)
+                gate_parked(i, 0, nc.vector)
+                gate_parked(i, 1, nc.gpsimd)
                 if following is not None:
-                    gate_parked(i, 0, nc.vector)
-                    gate_parked(i, 1, nc.gpsimd)
                     gate_in_psum(i, COMP - 1)
             if again:
                 multiply_y1(following, PARKED, COMP, again=True)
@@ -509,7 +513,7 @@ def tile_intermodule_pa_kernel(tc, x, w1_l0, w1_l1, w2_l0, w2_l1, out):
             gate_y0(i, 1)
             if second is not None:
                 multiply_y0(second, 1, 2)
-            if before is not None and following is not None:
+            if before is not None and following is not None and i not in KEPT:
                 if before in VECTOR_FINISHES:
                     finish_o1(before, 0, nc.vector)
                 finish_o1(before, 1, nc.vector)
@@ -519,17 +523,19 @@ def tile_intermodule_pa_kernel(tc, x, w1_l0, w1_l1, w2_l0, w2_l1, out):
                 multiply_o0(i)
                 finish_o0(i)
                 gate_in_psum(i, COMP - 1)
-                gate_parked(i, 0, nc.vector)
-                gate_parked(i, 1, nc.vector)
                 quantise_h(i, 0, H0_PLACE)
             else:
                 quantise_h(i, 0, 4)
                 multiply_o0(i)
+            if before in KEPT and i in KEPT:
+                finish_o1(before, 1, nc.vector)
+                store_o1(before)
             multiply_o1(i, (0, 2))
             quantise_c1(i)
             multiply_o1(i, (1,))
             if second is not None:
                 abs_y0(second)
         finish_o1(order[-1], 0, nc.scalar)
+        store_o1(order[-1], 0, 1)
         finish_o1(order[-1], 1, nc.vector)
-        store_o1(order[-1])
+        store_o1(order[-1], 1, 2)

@@ -34,6 +34,7 @@ VECTOR_COPIES = [1, 2]
 SCALAR_PARKS = []
 VECTOR_FINISHES = [0, 2]
 GPSIMD_SUMS = [0, 1, 2, 3, 4]
+VECTOR_COLUMNS = 256
 WARM_UP = 18
 TINY = 1e-30
 
@@ -93,7 +94,7 @@ def tile_intermodule_pa_kernel(tc, x, w1_l0, w1_l1, w2_l0, w2_l1, out):
         w1_grp = keep.tile([P, F0, PACK], BF16, name="w1_grp", align_bytes=64)
         w1_codes = keep.tile([P, F0], U32, name="w1_codes", align_bytes=64)
         w1_scales = keep.tile([P, F0], U8, name="w1_scales", align_bytes=64)
-        w2_grp = keep.tile([P, PASSES0, U0, PACK], BF16, name="w2_grp", align_bytes=64)
+        w2_grp = keep.tile([P, U0, PACK], BF16, name="w2_grp", align_bytes=64)
         w2_codes = keep.tile([P, PASSES0, U0], U32, name="w2_codes", align_bytes=64)
         w2_scales = keep.tile([P, PASSES0, U0], U8, name="w2_scales", align_bytes=64)
         v2_grp = keep.tile([P, U1, PACK], BF16, name="v2_grp", align_bytes=64)
@@ -315,9 +316,12 @@ def tile_intermodule_pa_kernel(tc, x, w1_l0, w1_l1, w2_l0, w2_l1, out):
         def h1_values(i, c):
             return c1_grp[i] if c == 1 else h_grp[i][:, H1_PLACE[c], :]
 
-        def gate_parked(i, c, engine):
+        def gate_parked(i, c, engine, first=0, end=F1):
             engine.tensor_tensor(
-                out=h1_values(i, c), in0=y1_sb[:, i, c, :], in1=gates[:, i, PASSES0, :], op=ALU.mult
+                out=h1_values(i, c)[:, first:end],
+                in0=y1_sb[:, i, c, first:end],
+                in1=gates[:, i, PASSES0, first:end],
+                op=ALU.mult,
             )
 
         def gate_in_psum(i, c):
@@ -410,11 +414,22 @@ def tile_intermodule_pa_kernel(tc, x, w1_l0, w1_l1, w2_l0, w2_l1, out):
             cols = slice(a * half, (a + 1) * half)
             quantise(w1_codes[:, cols], w1_scales[:, cols], w1_grp[:, cols, :].rearrange("p w t -> p (w t)"))
 
-        def regroup_w2(g):
-            regroup(w2_grp[:, g, :, :], w2_raw[:, g * PACK : (g + 1) * PACK, :])
+        def regroup_w2(g, on_gpsimd=False):
+            raw = w2_raw[:, g * PACK : (g + 1) * PACK, :]
+            if on_gpsimd:
+                nc.gpsimd.tensor_scalar(
+                    out=w2_grp[:],
+                    in0=raw.rearrange("p t w -> p w t"),
+                    scalar1=1.0,
+                    scalar2=0.0,
+                    op0=ALU.mult,
+                    op1=ALU.add,
+                )
+            else:
+                regroup(w2_grp[:], raw)
 
         def quantise_w2(g):
-            quantise(w2_codes[:, g, :], w2_scales[:, g, :], w2_grp[:, g, :, :].rearrange("p w t -> p (w t)"))
+            quantise(w2_codes[:, g, :], w2_scales[:, g, :], w2_grp[:].rearrange("p w t -> p (w t)"))
 
         preparation = {
             4: lambda: regroup_w1(0),
@@ -466,10 +481,9 @@ def tile_intermodule_pa_kernel(tc, x, w1_l0, w1_l1, w2_l0, w2_l1, out):
         turn_root(order[0])
         root(TILES - 1)
         turn_root(order[1])
-        for g in range(PASSES0):
-            regroup_w2(g)
-        for g in range(PASSES0):
-            quantise_w2(g)
+        regroup_w2(0)
+        quantise_w2(0)
+        regroup_w2(1, on_gpsimd=True)
         sigmoid_turned(order[0])
         sigmoid_turned(order[1])
         multiply_y0(order[0])
@@ -482,6 +496,7 @@ def tile_intermodule_pa_kernel(tc, x, w1_l0, w1_l1, w2_l0, w2_l1, out):
             if i == order[0]:
                 multiply_y0(order[1])
                 abs_y0(order[1])
+        quantise_w2(1)
 
         for j, i in enumerate(order):
             before = order[j - 1] if j > 0 else None
@@ -501,8 +516,9 @@ def tile_intermodule_pa_kernel(tc, x, w1_l0, w1_l1, w2_l0, w2_l1, out):
                     store_o1(before)
             if i not in KEPT:
                 open_tile(i)
-                gate_parked(i, 0, nc.vector)
+                gate_parked(i, 0, nc.vector, 0, VECTOR_COLUMNS)
                 gate_parked(i, 1, nc.gpsimd)
+                gate_parked(i, 0, nc.gpsimd, VECTOR_COLUMNS, F1)
                 if following is not None:
                     gate_in_psum(i, COMP - 1)
             if again:

import math

import concourse.mybir as mybir
from concourse.masks import make_identity

F32 = mybir.dt.float32
BF16 = mybir.dt.bfloat16
U32 = mybir.dt.uint32
U8 = mybir.dt.uint8
FP8X4 = mybir.dt.float8_e4m3fn_x4
FUNC = mybir.ActivationFunctionType
ALU = mybir.AluOpType

P = 128
PACK = 4
ROWS = 1024
TILES = ROWS // P
U0, F0 = 512, 1024
U1, F1, COMP = 256, 512, 3
X_COLS = U0 + U1 * COMP
K1 = U1 // P
PASSES0 = F0 // (P * PACK)
HALVES = U1 // P

S_Y0 = 1.0 / math.sqrt(U0)
S_O0 = 1.0 / math.sqrt(F0)
S_Y1 = 1.0 / math.sqrt(U1)
S_O1 = 1.0 / math.sqrt(F1)
KEPT = [6, 7]
PARKED = 2
TENSOR_SUMS = [6, 7]
LATE_ROOTS = [4, 5]
VECTOR_COPIES = [1, 2]
SCALAR_PARKS = []
VECTOR_FINISHES = [0, 2]
GPSIMD_SUMS = [0, 1, 2, 3, 4]
VECTOR_COLUMNS = 256
WARM_UP = 18
TINY = 1e-30

FLOPS = 2 * ROWS * (U0 * F0 + F0 * U0 + COMP * U1 * F1 + COMP * F1 * U1)


def tile_intermodule_pa_kernel(tc, x, w1_l0, w1_l1, w2_l0, w2_l1, out):
    nc = tc.nc
    with tc.tile_pool(name="keep", bufs=1) as keep, tc.tile_pool(name="two", bufs=2) as two, tc.tile_pool(
        name="three", bufs=3
    ) as three, tc.psum_pool(name="psum", bufs=1) as psum, tc.manual_schedule():

        def bank(number, shape, dtype, name):
            return psum.tile(shape, dtype, tag="bank%d" % number, name=name)

        x_sb = [keep.tile([P, X_COLS], BF16, name="x_sb%d" % i) for i in range(TILES)]
        w1l1_sb = keep.tile([P, K1, F1], BF16, name="w1l1_sb")
        w1_raw = keep.tile([P, PACK, F0], BF16, name="w1_raw")
        w2_raw = keep.tile([P, PASSES0 * PACK, U0], BF16, name="w2_raw")
        v2_raw = keep.tile([P, PACK, U1], BF16, name="v2_raw")

        def load_x(i, first=0, end=X_COLS):
            nc.sync.dma_start(out=x_sb[i][:, first:end], in_=x[i * P : (i + 1) * P, first:end])

        def load_w1(first, end):
            for u in range(2):
                nc.sync.dma_start(
                    out=w1_raw[:, 2 * u : 2 * u + 2, first:end],
                    in_=w1_l0[256 * u : 256 * (u + 1), first:end].rearrange("(p e) f -> p e f", e=2),
                )

        load_x(0, U0, X_COLS)
        nc.sync.dma_start(out=w1l1_sb[:], in_=w1_l1.rearrange("(k p) v -> p k v", p=P))
        load_x(1, U0, X_COLS)
        nc.sync.dma_start(out=v2_raw[:], in_=w2_l1.rearrange("(t p) w -> p t w", p=P))
        load_x(2)
        for i in range(2):
            load_x(i, 0, U0)
        load_x(3)
        load_w1(0, F0 // 2)
        load_x(4)
        load_w1(F0 // 2, F0)
        for i in range(5, TILES):
            load_x(i)
        nc.sync.dma_start(out=w2_raw[:], in_=w2_l0.rearrange("(a p) j -> p a j", p=P))

        tiny = keep.tile([P, 1], F32, name="tiny")
        nc.vector.memset(tiny[:], TINY)
        first_root = keep.tile([P, 1], F32, name="first_root")
        nc.scalar.activation(out=first_root[:], in_=tiny[:], func=FUNC.Sqrt)

        ident_f32 = keep.tile([P, P], F32, name="ident_f32")
        ident_bf16 = keep.tile([P, P], BF16, name="ident_bf16")
        make_identity(nc, ident_bf16[:])
        make_identity(nc, ident_f32[:])

        w1_grp = keep.tile([P, F0, PACK], BF16, name="w1_grp", align_bytes=64)
        w1_codes = keep.tile([P, F0], U32, name="w1_codes", align_bytes=64)
        w1_scales = keep.tile([P, F0], U8, name="w1_scales", align_bytes=64)
        w2_grp = keep.tile([P, U0, PACK], BF16, name="w2_grp", align_bytes=64)
        w2_codes = keep.tile([P, PASSES0, U0], U32, name="w2_codes", align_bytes=64)
        w2_scales = keep.tile([P, PASSES0, U0], U8, name="w2_scales", align_bytes=64)
        v2_grp = keep.tile([P, U1, PACK], BF16, name="v2_grp", align_bytes=64)
        v2_codes = keep.tile([P, U1], U32, name="v2_codes", align_bytes=64)
        v2_scales = keep.tile([P, U1], U8, name="v2_scales", align_bytes=64)
        x0_grp = keep.tile([P, TILES, P * PACK], BF16, name="x0_grp", align_bytes=64)
        x0_codes = keep.tile([P, TILES, P], U32, name="x0_codes", align_bytes=64)
        x0_scales = keep.tile([P, TILES, P], U8, name="x0_scales", align_bytes=64)
        y1_sb = keep.tile([P, TILES - len(KEPT), PARKED, F1], F32, name="y1_sb", align_bytes=64)
        gates = keep.tile([P, TILES, PASSES0 + 1, F1], F32, name="gates")

        def regroup(grouped, raw):
            nc.vector.tensor_copy(
                out=grouped.rearrange("p (c i) t -> p c t i", i=4),
                in_=raw.rearrange("p t (c i) -> p c t i", i=4),
            )

        def quantise(codes, scales, grouped):
            nc.vector.quantize_mx(out=codes.bitcast(FP8X4), scales=scales, in_=grouped)

        warm_in = keep.tile([P, P * PACK], BF16, name="warm_in", align_bytes=64)
        warm_codes = keep.tile([P, P], U32, name="warm_codes", align_bytes=64)
        warm_scales = keep.tile([P, P], U8, name="warm_scales", align_bytes=64)
        nc.vector.memset(warm_in[:], 0.0)
        quantise(warm_codes[:], warm_scales[:], warm_in[:])
        warm_ps = bank(7, [P, PACK, P], F32, "warm_ps")
        for i in range(WARM_UP):
            nc.tensor.matmul_mx(
                out=warm_ps[:, i % PACK, :],
                lhsT=warm_codes[:].bitcast(FP8X4),
                lhsT_scale=warm_scales[:],
                rhs=warm_codes[:].bitcast(FP8X4),
                rhs_scale=warm_scales[:],
                start=True,
                stop=True,
            )

        x0_ps = {}
        x1_ps = {}
        x1t = {}
        y1_bank = {}
        squares = {}
        sums = {}
        root_rows = {}
        turned = {}

        def transpose_x1(i, c, x1_ps, place):
            view = x_sb[i][:, U0:X_COLS].rearrange("p (k u c) -> p k c u", k=K1, u=P, c=COMP)
            for k in range(K1):
                nc.tensor.transpose(x1_ps[:, place * K1 + k, :], view[:, k, c, :], ident_bf16[:])

        def turn_x0(first):
            x0_ps[first] = bank(0, [P, 2, 2, P], F32, "x0_ps")
            for i in range(2):
                words = x_sb[first + i][:].bitcast(F32)
                for u in range(2):
                    nc.tensor.transpose(x0_ps[first][:, i, u, :], words[:, u * P : (u + 1) * P], ident_f32[:])

        def copy_x0(first):
            nc.vector.tensor_copy(
                out=x0_grp[:, first : first + 2, :].bitcast(F32).rearrange("p i (n u) -> p i n u", u=2),
                in_=x0_ps[first][:].rearrange("p i u n -> p i n u"),
            )

        def turn_x1(i):
            x1_ps[i] = bank(1, [P, COMP * K1, P], BF16, "x1_ps")
            for c in range(COMP):
                transpose_x1(i, c, x1_ps[i], c)

        def copy_x1(i):
            x1t[i] = keep.tile([P, COMP * K1, P], BF16, name="x1t%d" % i)
            if i in VECTOR_COPIES:
                nc.vector.tensor_copy(out=x1t[i][:], in_=x1_ps[i][:])
            else:
                nc.scalar.copy(out=x1t[i][:], in_=x1_ps[i][:])

        def bring_first_x1():
            first_ps = [bank(1, [P, K1, P], BF16, "first_ps"), bank(0, [P, 2 * K1, P], BF16, "second_ps")]
            x1t[0] = keep.tile([P, COMP * K1, P], BF16, name="x1t0")
            transpose_x1(0, 0, first_ps[0], 0)
            nc.scalar.copy(out=x1t[0][:, 0:K1, :], in_=first_ps[0][:])
            for c in range(1, COMP):
                transpose_x1(0, c, first_ps[1], c - 1)
            nc.vector.tensor_copy(out=x1t[0][:, K1:, :], in_=first_ps[1][:])

        def multiply_y1(i, first=0, end=COMP, again=False):
            for c in range(first, end):
                y1_bank[i, c] = bank(5 if again else 2 + COMP * (i % 2) + c, [P, PACK, P], F32, "y1_ps")
                for t in range(PACK):
                    for k in range(K1):
                        nc.tensor.matmul(
                            y1_bank[i, c][:, t, :],
                            lhsT=w1l1_sb[:, k, t * P : (t + 1) * P],
                            rhs=x1t[i][:, c * K1 + k, :],
                            start=(k == 0),
                            stop=(k == K1 - 1),
                        )

        def park_y1(i, c, on_scalar):
            to_sbuf = y1_sb[:, i, c, :].rearrange("p (n t) -> p n t", t=PACK)
            from_psum = y1_bank[i, c][:].rearrange("p t n -> p n t")
            if on_scalar:
                nc.scalar.activation(out=to_sbuf, in_=from_psum, func=FUNC.Copy, scale=S_Y1)
            else:
                nc.vector.tensor_scalar(out=to_sbuf, in0=from_psum, scalar1=S_Y1, scalar2=None, op0=ALU.mult)

        def square_y1(i):
            squares[i] = three.tile([P, COMP, F1], F32, name="squares")
            for c in range(COMP):
                from_psum = y1_bank[i, c][:]
                nc.scalar.activation(
                    out=squares[i][:, c, :].rearrange("p (t n) -> p t n", t=PACK)
                    if i in TENSOR_SUMS
                    else squares[i][:, c, :].rearrange("p (n t) -> p n t", t=PACK),
                    in_=from_psum if i in TENSOR_SUMS else from_psum.rearrange("p t n -> p n t"),
                    func=FUNC.Square,
                    scale=S_Y1,
                )

        def add_squares_first(i):
            nc.vector.tensor_tensor(
                out=gates[:, i, PASSES0, :], in0=squares[i][:, 0, :], in1=squares[i][:, 1, :], op=ALU.add
            )

        def add_squares_last(i, engine):
            engine.tensor_tensor(out=gates[:, i, PASSES0, :], in0=gates[:, i, PASSES0, :], in1=squares[i][:, 2, :], op=ALU.add)

        def sum_on_tensor(i):
            sums[i] = bank(i % 2 if i in KEPT else 0, [P, PACK, P], F32, "sums_ps")
            for t in range(PACK):
                for c in range(COMP):
                    nc.tensor.matmul(
                        sums[i][:, t, :],
                        lhsT=squares[i][:, c, t * P : (t + 1) * P],
                        rhs=ident_f32[:],
                        start=(c == 0),
                        stop=(c == COMP - 1),
                        is_transpose=True,
                    )

        def root(i):
            if i in TENSOR_SUMS:
                root_rows[i] = keep.tile([P, PACK, P], F32, name="root_rows%d" % i)
                nc.scalar.activation(out=root_rows[i][:], in_=sums[i][:], func=FUNC.Sqrt, bias=tiny[:])
            else:
                nc.scalar.activation(out=gates[:, i, PASSES0, :], in_=gates[:, i, PASSES0, :], func=FUNC.Sqrt, bias=tiny[:])

        def turn_root(i):
            turned[i] = bank(i % 2 if i in KEPT else 5, [P, PACK, P], F32, "turned_ps")
            for t in range(PACK):
                nc.tensor.transpose(turned[i][:, t, :], root_rows[i][:, t, :], ident_f32[:])

        def quantise_x0(first, count):
            quantise(
                x0_codes[:, first : first + count, :].rearrange("p i n -> p (i n)"),
                x0_scales[:, first : first + count, :].rearrange("p i n -> p (i n)"),
                x0_grp[:, first : first + count, :].rearrange("p i f -> p (i f)"),
            )

        y0_bank = {}
        h_grp = {}
        h_codes = {}
        h_scales = {}
        c1_grp = {}
        H1_PLACE = (0, 4, 1)
        H0_PLACE = 2
        o0_bank = {}
        o1_bank = {}
        staged = {}
        order = KEPT + list(range(TILES - len(KEPT)))
        place = {i: j for j, i in enumerate(order)}
        Y0_BANKS = ((0, 1), (2, 3))
        O1_BANKS = (6, 7)

        def multiply_y0(i, first=0, end=PASSES0):
            for g in range(first, end):
                y0_bank[i, g] = bank(Y0_BANKS[place[i] % 2][g], [P, PACK, P], F32, "y0_ps")
                for t in range(PACK):
                    cols = slice((g * PACK + t) * P, (g * PACK + t + 1) * P)
                    nc.tensor.matmul_mx(
                        out=y0_bank[i, g][:, t, :],
                        lhsT=w1_codes[:, cols].bitcast(FP8X4),
                        lhsT_scale=w1_scales[:, cols],
                        rhs=x0_codes[:, i, :].bitcast(FP8X4),
                        rhs_scale=x0_scales[:, i, :],
                        start=True,
                        stop=True,
                    )

        def abs_y0(i):
            for g in range(PASSES0):
                nc.scalar.activation(
                    out=gates[:, i, g, :].rearrange("p (n t) -> p n t", t=PACK),
                    in_=y0_bank[i, g][:].rearrange("p t n -> p n t"),
                    func=FUNC.Abs,
                    scale=S_Y0,
                )

        def sigmoids(i, first=0, end=PASSES0 + 1):
            nc.scalar.activation(out=gates[:, i, first:end, :], in_=gates[:, i, first:end, :], func=FUNC.Sigmoid)

        def sigmoid_turned(i):
            nc.scalar.activation(
                out=gates[:, i, PASSES0, :].rearrange("p (n t) -> p n t", t=PACK),
                in_=turned[i][:].rearrange("p t n -> p n t"),
                func=FUNC.Sigmoid,
            )

        def open_tile(i):
            h_grp[i] = two.tile([P, 4, F1], BF16, name="h_grp", align_bytes=64)
            h_codes[i] = two.tile([P, 5, P], U32, name="h_codes", align_bytes=64)
            h_scales[i] = two.tile([P, 5, P], U8, name="h_scales", align_bytes=64)
            if i in KEPT:
                c1_kept = two.tile([P, F1], BF16, name="c1_kept", align_bytes=64)
                c1_grp[i] = c1_kept[:]
            else:
                c1_grp[i] = y1_sb[:, i, 0, :].bitcast(BF16)[:, 0:F1]

        def h1_values(i, c):
            return c1_grp[i] if c == 1 else h_grp[i][:, H1_PLACE[c], :]

        def gate_parked(i, c, engine, first=0, end=F1):
            engine.tensor_tensor(
                out=h1_values(i, c)[:, first:end],
                in0=y1_sb[:, i, c, first:end],
                in1=gates[:, i, PASSES0, first:end],
                op=ALU.mult,
            )

        def gate_in_psum(i, c):
            nc.vector.scalar_tensor_tensor(
                out=h1_values(i, c).rearrange("p (n t) -> p n t", t=PACK),
                in0=y1_bank[i, c][:].rearrange("p t n -> p n t"),
                scalar=S_Y1,
                in1=gates[:, i, PASSES0, :].rearrange("p (n t) -> p n t", t=PACK),
                op0=ALU.mult,
                op1=ALU.mult,
            )

        def gate_y0(i, g):
            nc.vector.scalar_tensor_tensor(
                out=h_grp[i][:, H0_PLACE + g, :].rearrange("p (n t) -> p n t", t=PACK),
                in0=y0_bank[i, g][:].rearrange("p t n -> p n t"),
                scalar=S_Y0,
                in1=gates[:, i, g, :].rearrange("p (n t) -> p n t", t=PACK),
                op0=ALU.mult,
                op1=ALU.mult,
            )

        def quantise_h(i, first, count):
            quantise(
                h_codes[i][:, first : first + count, :].rearrange("p c n -> p (c n)"),
                h_scales[i][:, first : first + count, :].rearrange("p c n -> p (c n)"),
                h_grp[i][:, first : first + count, :].rearrange("p c f -> p (c f)"),
            )

        def quantise_c1(i):
            quantise(h_codes[i][:, H1_PLACE[1], :], h_scales[i][:, H1_PLACE[1], :], c1_grp[i])

        def multiply_o1(i, components):
            for h in range(HALVES):
                if (i, h) not in o1_bank:
                    o1_bank[i, h] = bank(O1_BANKS[h], [P, COMP, P], F32, "o1_ps")
                for c in components:
                    nc.tensor.matmul_mx(
                        out=o1_bank[i, h][:, c, :],
                        lhsT=h_codes[i][:, H1_PLACE[c], :].bitcast(FP8X4),
                        lhsT_scale=h_scales[i][:, H1_PLACE[c], :],
                        rhs=v2_codes[:, h * P : (h + 1) * P].bitcast(FP8X4),
                        rhs_scale=v2_scales[:, h * P : (h + 1) * P],
                        start=True,
                        stop=True,
                    )

        def multiply_o0(i):
            o0_bank[i] = bank(4, [P, U0], F32, "o0_ps")
            for g in range(PASSES0):
                nc.tensor.matmul_mx(
                    out=o0_bank[i][:],
                    lhsT=h_codes[i][:, H0_PLACE + g, :].bitcast(FP8X4),
                    lhsT_scale=h_scales[i][:, H0_PLACE + g, :],
                    rhs=w2_codes[:, g, :].bitcast(FP8X4),
                    rhs_scale=w2_scales[:, g, :],
                    start=(g == 0),
                    stop=(g == PASSES0 - 1),
                )

        def o1_views(i, h):
            first = U0 + h * P * COMP
            return (
                staged[i][:, first : first + P * COMP].rearrange("p (w c) -> p w c", c=COMP),
                o1_bank[i, h][:].rearrange("p c w -> p w c"),
            )

        def finish_o0(i):
            staged[i] = three.tile([P, X_COLS], F32, name="staged")
            nc.scalar.activation(out=staged[i][:, 0:U0], in_=o0_bank[i][:], func=FUNC.Copy, scale=S_O0)
            nc.sync.dma_start(out=out[i * P : (i + 1) * P, 0:U0], in_=staged[i][:, 0:U0])

        def finish_o1(i, h, engine):
            to_sbuf, from_psum = o1_views(i, h)
            if engine is nc.scalar:
                nc.scalar.activation(out=to_sbuf, in_=from_psum, func=FUNC.Copy, scale=S_O1)
            else:
                nc.vector.tensor_scalar(out=to_sbuf, in0=from_psum, scalar1=S_O1, scalar2=None, op0=ALU.mult)

        def store_o1(i, first=0, end=HALVES):
            cols = slice(U0 + first * P * COMP, U0 + end * P * COMP)
            nc.sync.dma_start(out=out[i * P : (i + 1) * P, cols], in_=staged[i][:, cols])

        half = F0 // 2

        def regroup_w1(a):
            regroup(w1_grp[:, a * half : (a + 1) * half, :], w1_raw[:, :, a * half : (a + 1) * half])

        def quantise_w1(a):
            cols = slice(a * half, (a + 1) * half)
            quantise(w1_codes[:, cols], w1_scales[:, cols], w1_grp[:, cols, :].rearrange("p w t -> p (w t)"))

        def regroup_w2(g, on_gpsimd=False):
            raw = w2_raw[:, g * PACK : (g + 1) * PACK, :]
            if on_gpsimd:
                nc.gpsimd.tensor_scalar(
                    out=w2_grp[:],
                    in0=raw.rearrange("p t w -> p w t"),
                    scalar1=1.0,
                    scalar2=0.0,
                    op0=ALU.mult,
                    op1=ALU.add,
                )
            else:
                regroup(w2_grp[:], raw)

        def quantise_w2(g):
            quantise(w2_codes[:, g, :], w2_scales[:, g, :], w2_grp[:].rearrange("p w t -> p (w t)"))

        preparation = {
            4: lambda: regroup_w1(0),
            5: lambda: regroup_w1(1),
            6: lambda: (quantise_x0(0, TILES // 2), quantise_w1(0)),
            7: lambda: (quantise_x0(TILES // 2, TILES // 2), quantise_w1(1)),
        }

        bring_first_x1()
        multiply_y1(0, 0, 1)
        turn_x1(1)
        copy_x1(1)
        multiply_y1(0, 1, COMP)
        regroup(v2_grp[:], v2_raw[:])
        for i in range(TILES):
            if i == 1:
                quantise(v2_codes[:], v2_scales[:], v2_grp[:].rearrange("p w t -> p (w t)"))
            if i + 2 < TILES:
                turn_x1(i + 2)
            if i + 1 < TILES:
                multiply_y1(i + 1)
            if i < TILES // 2:
                turn_x0(2 * i)
            if i - 1 in KEPT:
                sum_on_tensor(i - 1)
            square_y1(i)
            if i - 1 in GPSIMD_SUMS:
                add_squares_first(i - 1)
                add_squares_last(i - 1, nc.gpsimd)
            if i not in KEPT:
                for c in range(PARKED):
                    park_y1(i, c, c == PARKED - 1 and i in SCALAR_PARKS)
            if i + 2 < TILES:
                copy_x1(i + 2)
            if i >= 2 and i - 2 not in LATE_ROOTS + TENSOR_SUMS:
                root(i - 2)
            if i not in TENSOR_SUMS + GPSIMD_SUMS:
                add_squares_first(i)
            if i < TILES // 2:
                copy_x0(2 * i)
            if i in preparation:
                preparation[i]()
            if i not in TENSOR_SUMS + GPSIMD_SUMS:
                add_squares_last(i, nc.vector)
        sum_on_tensor(TILES - 1)
        for i in LATE_ROOTS:
            root(i)
        root(TILES - 2)
        turn_root(order[0])
        root(TILES - 1)
        turn_root(order[1])
        regroup_w2(0)
        quantise_w2(0)
        regroup_w2(1, on_gpsimd=True)
        sigmoid_turned(order[0])
        sigmoid_turned(order[1])
        multiply_y0(order[0])
        abs_y0(order[0])
        sigmoids(order[0], 0, PASSES0)
        for i in KEPT:
            open_tile(i)
            for c in range(COMP):
                gate_in_psum(i, c)
            if i == order[0]:
                multiply_y0(order[1])
                abs_y0(order[1])
        quantise_w2(1)

        for j, i in enumerate(order):
            before = order[j - 1] if j > 0 else None
            following = order[j + 1] if j + 1 < TILES else None
            second = order[j + 2] if j + 2 < TILES else None
            again = following is not None and following not in KEPT
            if again:
                sigmoids(following, PASSES0, PASSES0 + 1)
            if following is not None:
                sigmoids(following, 0, PASSES0)
            if before is not None:
                finish_o0(before)
                if before not in VECTOR_FINISHES:
                    finish_o1(before, 0, nc.scalar)
                if following is None:
                    finish_o1(before, 1, nc.scalar)
                    store_o1(before)
            if i not in KEPT:
                open_tile(i)
                gate_parked(i, 0, nc.vector, 0, VECTOR_COLUMNS)
                gate_parked(i, 1, nc.gpsimd)
                gate_parked(i, 0, nc.gpsimd, VECTOR_COLUMNS, F1)
                if following is not None:
                    gate_in_psum(i, COMP - 1)
            if again:
                multiply_y1(following, PARKED, COMP, again=True)
            gate_y0(i, 0)
            if second is not None:
                multiply_y0(second, 0, 1)
            gate_y0(i, 1)
            if second is not None:
                multiply_y0(second, 1, 2)
            if before is not None and following is not None and i not in KEPT:
                if before in VECTOR_FINISHES:
                    finish_o1(before, 0, nc.vector)
                finish_o1(before, 1, nc.vector)
                store_o1(before)
            if following is None:
                quantise_h(i, H0_PLACE, PASSES0)
                multiply_o0(i)
                finish_o0(i)
                gate_in_psum(i, COMP - 1)
                quantise_h(i, 0, H0_PLACE)
            else:
                quantise_h(i, 0, 4)
                multiply_o0(i)
            if before in KEPT and i in KEPT:
                finish_o1(before, 1, nc.vector)
                store_o1(before)
            multiply_o1(i, (0, 2))
            quantise_c1(i)
            multiply_o1(i, (1,))
            if second is not None:
                abs_y0(second)
        finish_o1(order[-1], 0, nc.scalar)
        store_o1(order[-1], 0, 1)
        finish_o1(order[-1], 1, nc.vector)
        store_o1(order[-1], 1, 2)
